import numpy as np
import ml_dtypes


BF16 = ml_dtypes.bfloat16


def bf(x):
    return np.asarray(x, np.float32).astype(BF16)


def f64(x):
    return np.asarray(x).astype(np.float64)


E2M1 = np.array([0.0, 0.5, 1.0, 1.5, 2.0, 3.0, 4.0, 6.0, -0.0, -0.5, -1.0, -1.5, -2.0, -3.0, -4.0, -6.0])


def pack_weight(w, fmt):
    k, n = w.shape
    w = f64(bf(w)).reshape(k // 32, 32, n)
    amax = np.abs(w).max(1)
    if fmt == "e4m3":
        byte = np.frexp(amax)[1] - 1 + 127 - 7
    else:
        mant, ex = np.frexp(amax / 6.0)
        byte = np.where(mant > 0.5, ex, ex - 1) + 127
    byte = np.clip(np.where(amax > 0, byte, 1), 1, 254)
    scaled = (w * np.exp2(127.0 - byte)[:, None, :]).reshape(k, n).astype(np.float32)
    by_word = np.ascontiguousarray(scaled.reshape(k // 512, 128, 4, n).transpose(0, 1, 3, 2))
    if fmt == "e4m3":
        words = by_word.astype(ml_dtypes.float8_e4m3fn).view(np.uint8)
    else:
        c = by_word.astype(ml_dtypes.float4_e2m1fn).view(np.uint8) & 0xF
        words = c[..., 0::2] | (c[..., 1::2] << 4)
    return np.ascontiguousarray(words), np.ascontiguousarray(byte.astype(np.uint8).reshape(k // 512, 16, n))


def unpack_weight(words, scales, fmt):
    g, p, n, _ = words.shape
    if fmt == "e4m3":
        vals = np.ascontiguousarray(words).view(ml_dtypes.float8_e4m3fn).astype(np.float64)
    else:
        nib = np.empty((g, p, n, 4), np.uint8)
        nib[..., 0::2] = words & 0xF
        nib[..., 1::2] = words >> 4
        vals = E2M1[nib]
    vals = vals * np.repeat(np.exp2(scales.astype(np.float64) - 127.0), 8, axis=1)[..., None]
    return vals.transpose(0, 1, 3, 2).reshape(g * 512, n)

def pack4(w):
    words, scales = pack_weight(w, "e2m1")
    return words.reshape(words.shape[0], 128, -1), scales


def unpack4(words, scales):
    return unpack_weight(words.reshape(words.shape[0], 128, -1, 2), scales, "e2m1")


def kspread(k):
    return np.exp2(np.repeat(np.random.randint(-6, 7, k // 32), 32).astype(np.float64))


B, C, HH, WW, NH, HD, F = 16, 1024, 16, 16, 8, 128, 4096
EPS = 1e-5


def layer_norm(v, w, b):
    mu = v.mean(-1, keepdims=True)
    var = ((v - mu) ** 2).mean(-1, keepdims=True)
    return (v - mu) * (1.0 / np.sqrt(var + EPS)) * w + b


def setup_inputs():
    s = kspread(F)
    h = np.maximum(np.random.standard_normal((B, HH, WW, F)), 0.0) * 0.125 * s
    h_words, h_scales = pack4(np.ascontiguousarray(h.reshape(B * HH * WW, F).T))
    ffn2_w = np.random.standard_normal((C, F)) * 0.5 / np.sqrt(F) / s
    words, scales = pack4(np.ascontiguousarray(ffn2_w.T))
    return {"h_words": h_words,
            "h_scales": h_scales,
            "ffn2_w_words": words,
            "ffn2_w_scales": scales,
            "ffn2_b": bf(np.random.standard_normal(C) * 0.02),
            "scale_ffn": bf(0.1 * (1.0 + 0.1 * np.random.standard_normal(1))),
            "ln2_w": bf(1.0 + 0.1 * np.random.standard_normal(C)),
            "ln2_b": bf(0.1 * np.random.standard_normal(C)),
            "scale_norm2": bf(1.5 * (1.0 + 0.1 * np.random.standard_normal(1))),
            "x": bf(np.random.standard_normal((B, C, HH, WW)))}


def reference(h_words, h_scales, ffn2_w_words, ffn2_w_scales, ffn2_b, scale_ffn, ln2_w, ln2_b, scale_norm2, x):
    y2 = ((unpack4(h_words, h_scales).T.reshape(B, HH, WW, F) @ unpack4(ffn2_w_words, ffn2_w_scales)) + f64(ffn2_b)) * f64(scale_ffn)
    y2 = layer_norm(y2, f64(ln2_w), f64(ln2_b)) * f64(scale_norm2)
    out = np.maximum(y2 + f64(x).transpose(0, 2, 3, 1), 0.0)
    return out.transpose(0, 3, 1, 2)

@@ -1,0 +1,295 @@
+from contextlib import ExitStack
+
+import concourse.mybir as mybir
+from concourse.masks import make_identity
+
+FLOPS = 2 * 4096 * 4096 * 1024
+
+F32 = mybir.dt.float32
+BF16 = mybir.dt.bfloat16
+U8 = mybir.dt.uint8
+I32 = mybir.dt.int32
+FP4X4 = mybir.dt.float4_e2m1fn_x4
+ALU = mybir.AluOpType
+ACT = mybir.ActivationFunctionType
+
+P = 128
+PASSES = 8
+CHANNELS = 1024
+BANK = 512
+IMAGES = 16
+IMG_PIX = 256
+CT = CHANNELS // P
+EPS = 1e-5
+CHUNKS = ((0, 1), (1, 1), (2, 2), (4, 4), (8, 4), (12, 4))
+
+
+def tile_transformerconvblock_pc_kernel(
+    tc, h_words, h_scales, ffn2_w_words, ffn2_w_scales, ffn2_b, scale_ffn, ln2_w, ln2_b, scale_norm2, x, out
+):
+    nc = tc.nc
+
+    with ExitStack() as ctx:
+        keep = ctx.enter_context(tc.tile_pool(name="keep", bufs=1))
+        x_pool = ctx.enter_context(tc.tile_pool(name="x_pool", bufs=4))
+        y_pool = ctx.enter_context(tc.tile_pool(name="y_pool", bufs=3))
+        sq_pool = ctx.enter_context(tc.tile_pool(name="sq_pool", bufs=2))
+        st_pool = ctx.enter_context(tc.tile_pool(name="st_pool", bufs=4))
+        t_pool = ctx.enter_context(tc.tile_pool(name="t_pool", bufs=4))
+        o_pool = ctx.enter_context(tc.tile_pool(name="o_pool", bufs=3))
+        psum = ctx.enter_context(tc.psum_pool(name="psum", bufs=1))
+        ctx.enter_context(tc.manual_schedule())
+
+        hc = []
+        hp = []
+        where = {}
+        for ci, (first, count) in enumerate(CHUNKS):
+            hc.append(keep.tile([P, PASSES, 2 * IMG_PIX * count], U8, name="hc%d" % ci, align_bytes=64))
+            hp.append(keep.tile([P, PASSES, IMG_PIX * count], U8, name="hp%d" % ci, align_bytes=64))
+            for k in range(2 * count):
+                where[2 * first + k] = (ci, P * k)
+        wc = [keep.tile([P, 2, 2 * CHANNELS], U8, name="wc%d" % k, align_bytes=64) for k in range(4)]
+        wp = [keep.tile([P, 4, CHANNELS], U8, name="wp%d" % k, align_bytes=64) for k in range(2)]
+
+        brow = keep.tile([P, CHANNELS], BF16, name="brow")
+        ones = keep.tile([P, P], BF16, name="ones")
+        b_bc = keep.tile([P, CHANNELS], F32, name="b_bc")
+        ident = keep.tile([P, P], F32, name="ident")
+        one = keep.tile([P, 1], F32, name="one")
+        cneg = keep.tile([P, 1], F32, name="cneg")
+        warm = keep.tile([P, 1], F32, name="warm")
+        s_bf = keep.tile([P, 1], BF16, name="s_bf")
+        sn_bf = keep.tile([P, 1], BF16, name="sn_bf")
+        s2e = keep.tile([P, 1], F32, name="s2e")
+        ssn = keep.tile([P, 1], F32, name="ssn")
+        lnw_bf = keep.tile([P, CT], BF16, name="lnw_bf")
+        lnb_bf = keep.tile([P, CT], BF16, name="lnb_bf")
+        wv = keep.tile([P, CT], F32, name="wv")
+        bv = keep.tile([P, CT], F32, name="bv")
+
+        def load_codes(dst, src):
+            nc.sync.dma_start(out=dst.bitcast(I32), in_=src.rearrange("g p n -> p g n").bitcast(I32))
+
+        def load_scales(dst, src):
+            for q in range(4):
+                nc.sync.dma_start(
+                    out=dst[32 * q : 32 * q + 4, :, :].bitcast(I32),
+                    in_=src[:, 4 * q : 4 * q + 4, :].rearrange("g r n -> r g n").bitcast(I32),
+                )
+
+        def load_h_codes(ci):
+            first, count = CHUNKS[ci]
+            load_codes(hc[ci][:], h_words[:, :, 2 * IMG_PIX * first : 2 * IMG_PIX * (first + count)])
+
+        def load_h_scales(ci):
+            first, count = CHUNKS[ci]
+            load_scales(hp[ci], h_scales[:, :, IMG_PIX * first : IMG_PIX * (first + count)])
+
+        x_tiles = {}
+
+        def load_x(i):
+            x_tiles[i] = x_pool.tile([P, CT, IMG_PIX], BF16, name="x_t", tag="x_t")
+            nc.sync.dma_start(out=x_tiles[i][:], in_=x[i].rearrange("(ct p) h w -> p ct (h w)", p=P))
+
+        nc.vector.memset(hp[0][:].bitcast(I32), 0)
+        nc.vector.memset(wp[0][:].bitcast(I32), 0)
+        nc.vector.memset(wp[1][:].bitcast(I32), 0)
+        nc.vector.memset(brow[:], 0.0)
+        nc.vector.memset(ones[:], 1.0)
+        nc.vector.memset(one[:], 1.0)
+        nc.vector.memset(cneg[:], -1.0 / CHANNELS)
+        for ci in range(1, len(CHUNKS)):
+            nc.vector.memset(hp[ci][:].bitcast(I32), 0)
+        make_identity(nc, ident[:])
+        nc.scalar.activation(out=warm[:], in_=one[:], func=ACT.Sqrt)
+
+        load_h_scales(0)
+        load_h_codes(0)
+        load_codes(wc[0][:], ffn2_w_words[0:2])
+        load_scales(wp[0], ffn2_w_scales[0:4])
+        load_codes(wc[1][:], ffn2_w_words[2:4])
+        load_scales(wp[1], ffn2_w_scales[4:8])
+        nc.sync.dma_start(out=brow[0:1, :], in_=ffn2_b.rearrange("(o n) -> o n", o=1))
+        load_codes(wc[2][:], ffn2_w_words[4:6])
+        load_codes(wc[3][:], ffn2_w_words[6:8])
+        nc.sync.dma_start(out=s_bf[:], in_=scale_ffn.partition_broadcast(P))
+        nc.sync.dma_start(out=sn_bf[:], in_=scale_norm2.partition_broadcast(P))
+        load_h_codes(1)
+        load_h_scales(1)
+        with nc.allow_non_contiguous_dma(reason="one channel to a partition, 1024 elements, once"):
+            nc.sync.dma_start(out=lnw_bf[:], in_=ln2_w.rearrange("(ct p) -> p ct", p=P))
+            nc.sync.dma_start(out=lnb_bf[:], in_=ln2_b.rearrange("(ct p) -> p ct", p=P))
+        load_x(0)
+        load_h_codes(2)
+        load_h_scales(2)
+        load_x(1)
+        load_x(2)
+        load_h_codes(3)
+        load_h_scales(3)
+        load_x(3)
+        load_h_codes(4)
+        load_h_scales(4)
+        load_h_codes(5)
+        load_h_scales(5)
+
+        nc.vector.scalar_tensor_tensor(
+            out=s2e[:], in0=s_bf[:], scalar=1.0 / (CHANNELS * EPS), in1=s_bf[:], op0=ALU.mult, op1=ALU.mult
+        )
+        nc.vector.tensor_tensor(out=ssn[:], in0=s_bf[:], in1=sn_bf[:], op=ALU.mult)
+
+        acc = {}
+        y = {}
+        st = {}
+        t = {}
+        tp = {}
+        o = {}
+
+        def open_acc(tau):
+            for n in range(2):
+                bank = 2 * (tau % 2) + n
+                acc[(tau, n)] = psum.tile([P, BANK], F32, name="acc%d" % bank, tag="acc%d" % bank)
+
+        def mx_pass(tau, n, g):
+            ci, off = where[tau]
+            nc.tensor.matmul_mx(
+                out=acc[(tau, n)][:],
+                lhsT=hc[ci][:, g, 2 * off : 2 * off + 2 * P].bitcast(FP4X4),
+                lhsT_scale=hp[ci][:, g, off : off + P],
+                rhs=wc[g // 2][:, g % 2, 2 * BANK * n : 2 * BANK * (n + 1)].bitcast(FP4X4),
+                rhs_scale=wp[g // 4][:, g % 4, BANK * n : BANK * (n + 1)],
+                start=(g == 0),
+                stop=(g == PASSES - 1),
+            )
+
+        def mx(tau):
+            open_acc(tau)
+            for n in range(2):
+                for g in range(PASSES):
+                    mx_pass(tau, n, g)
+
+        def add_bias(tau):
+            y[tau] = y_pool.tile([P, CHANNELS], F32, name="y_t", tag="y_t")
+            st[tau] = st_pool.tile([P, 8], F32, name="st_t", tag="st_t")
+            for n in range(2):
+                cols = slice(BANK * n, BANK * (n + 1))
+                nc.vector.scalar_tensor_tensor(
+                    out=y[tau][:, cols],
+                    in0=acc[(tau, n)][:],
+                    scalar=1.0,
+                    in1=b_bc[:, cols],
+                    op0=ALU.mult,
+                    op1=ALU.add,
+                    accum_out=st[tau][:, n : n + 1],
+                )
+            nc.vector.scalar_tensor_tensor(
+                out=st[tau][:, 2:3],
+                in0=st[tau][:, 0:1],
+                scalar=st[tau][:, 1:2],
+                in1=cneg[:],
+                op0=ALU.add,
+                op1=ALU.mult,
+            )
+
+        def deviation(tau):
+            sq = sq_pool.tile([P, CHANNELS], BF16, name="sq_t", tag="sq_t")
+            nc.scalar.activation(
+                out=sq[:], in_=y[tau][:], func=ACT.Square, bias=st[tau][:, 2:3], scale=1.0, accum_out=st[tau][:, 3:4]
+            )
+            nc.scalar.activation(out=st[tau][:, 4:5], in_=st[tau][:, 3:4], func=ACT.Sqrt, bias=one[:], scale=s2e[:])
+
+        def normalise(tau):
+            nc.vector.reciprocal(out=st[tau][:, 5:6], in_=st[tau][:, 4:5])
+            t[tau] = t_pool.tile([P, CHANNELS], F32, name="t_t", tag="t_t")
+            nc.vector.tensor_scalar(
+                out=t[tau][:],
+                in0=y[tau][:],
+                scalar1=st[tau][:, 2:3],
+                scalar2=st[tau][:, 5:6],
+                op0=ALU.add,
+                op1=ALU.mult,
+            )
+
+        def transposes(i, halves):
+            for k in range(4):
+                tp[k] = psum.tile([P, 2, IMG_PIX], F32, name="tp%d" % k, tag="tp%d" % k)
+                for j in range(2):
+                    ct = 2 * k + j
+                    for h in halves:
+                        nc.tensor.transpose(
+                            tp[k][:, j, P * h : P * (h + 1)], t[2 * i + h][:, P * ct : P * (ct + 1)], ident[:]
+                        )
+
+        def finish(i, halves):
+            cols = slice(P * halves[0], P * (halves[-1] + 1))
+            if halves[0] == 0:
+                o[i] = o_pool.tile([P, CT, IMG_PIX], F32, name="o_t", tag="o_t")
+            for ct in range(CT):
+                nc.vector.scalar_tensor_tensor(
+                    out=o[i][:, ct, cols],
+                    in0=tp[ct // 2][:, ct % 2, cols],
+                    scalar=wv[:, ct : ct + 1],
+                    in1=x_tiles[i][:, ct, cols],
+                    op0=ALU.mult,
+                    op1=ALU.add,
+                )
+            for ct in range(CT):
+                nc.scalar.activation(
+                    out=o[i][:, ct, cols], in_=o[i][:, ct, cols], func=ACT.Relu, bias=bv[:, ct : ct + 1], scale=1.0
+                )
+            nc.sync.dma_start(
+                out=out[i].rearrange("(ct p) h w -> p ct (h w)", p=P)[:, :, cols], in_=o[i][:, :, cols]
+            )
+
+        open_acc(0)
+        open_acc(1)
+        for g in range(PASSES):
+            if g == 5:
+                for n in range(2):
+                    bb = psum.tile([P, BANK], F32, name="tp%d" % n, tag="tp%d" % n)
+                    nc.tensor.matmul(
+                        out=bb[:], lhsT=ones[:], rhs=brow[:, BANK * n : BANK * (n + 1)], start=True, stop=True
+                    )
+                    nc.scalar.copy(out=b_bc[:, BANK * n : BANK * (n + 1)], in_=bb[:])
+            for tau in range(2):
+                for n in range(2):
+                    mx_pass(tau, n, g)
+        add_bias(0)
+        deviation(0)
+        add_bias(1)
+        deviation(1)
+        normalise(0)
+        normalise(1)
+        nc.vector.tensor_scalar(
+            out=wv[:], in0=lnw_bf[:], scalar1=ssn[:], scalar2=EPS**-0.5, op0=ALU.mult, op1=ALU.mult
+        )
+        nc.vector.tensor_scalar_mul(out=bv[:], in0=lnb_bf[:], scalar1=sn_bf[:])
+
+        for i in range(1, IMAGES - 1):
+            mx(2 * i)
+            add_bias(2 * i)
+            deviation(2 * i)
+            normalise(2 * i)
+            mx(2 * i + 1)
+            add_bias(2 * i + 1)
+            deviation(2 * i + 1)
+            transposes(i - 1, (0, 1))
+            finish(i - 1, (0, 1))
+            if i + 3 < IMAGES:
+                load_x(i + 3)
+            normalise(2 * i + 1)
+
+        last = IMAGES - 1
+        mx(2 * last)
+        add_bias(2 * last)
+        deviation(2 * last)
+        transposes(last - 1, (0, 1))
+        finish(last - 1, (0, 1))
+        normalise(2 * last)
+        mx(2 * last + 1)
+        add_bias(2 * last + 1)
+        deviation(2 * last + 1)
+        transposes(last, (0,))
+        finish(last, (0,))
+        normalise(2 * last + 1)
+        transposes(last, (1,))
+        finish(last, (1,))

@@ -62,8 +62,9 @@ def tile_transformerconvblock_pc_kernel(
         sn_bf = keep.tile([P, 1], BF16, name="sn_bf")
         s2e = keep.tile([P, 1], F32, name="s2e")
         ssn = keep.tile([P, 1], F32, name="ssn")
-        lnw_bf = keep.tile([P, CT], BF16, name="lnw_bf")
-        lnb_bf = keep.tile([P, CT], BF16, name="lnb_bf")
+        vrows = keep.tile([P, P], BF16, name="vrows")
+        ident_bf = keep.tile([P, 32], BF16, name="ident_bf")
+        idle_rhs = keep.tile([P, BANK], BF16, name="idle_rhs")
         wv = keep.tile([P, CT], F32, name="wv")
         bv = keep.tile([P, CT], F32, name="bv")
 
@@ -93,14 +94,17 @@ def tile_transformerconvblock_pc_kernel(
 
         nc.vector.memset(hp[0][:].bitcast(I32), 0)
         nc.vector.memset(wp[0][:].bitcast(I32), 0)
+        nc.vector.memset(ones[:], 1.0)
+        nc.vector.memset(idle_rhs[:], 0.0)
         nc.vector.memset(wp[1][:].bitcast(I32), 0)
         nc.vector.memset(brow[:], 0.0)
-        nc.vector.memset(ones[:], 1.0)
+        nc.vector.memset(vrows[:], 0.0)
         nc.vector.memset(one[:], 1.0)
         nc.vector.memset(cneg[:], -1.0 / CHANNELS)
         for ci in range(1, len(CHUNKS)):
             nc.vector.memset(hp[ci][:].bitcast(I32), 0)
         make_identity(nc, ident[:])
+        nc.vector.tensor_copy(out=ident_bf[:], in_=ident[:, 0:32])
         nc.scalar.activation(out=warm[:], in_=one[:], func=ACT.Sqrt)
 
         load_h_scales(0)
@@ -110,15 +114,14 @@ def tile_transformerconvblock_pc_kernel(
         load_codes(wc[1][:], ffn2_w_words[2:4])
         load_scales(wp[1], ffn2_w_scales[4:8])
         nc.sync.dma_start(out=brow[0:1, :], in_=ffn2_b.rearrange("(o n) -> o n", o=1))
+        nc.sync.dma_start(out=vrows[0:CT, :], in_=ln2_w.rearrange("(r n) -> r n", r=CT))
+        nc.sync.dma_start(out=vrows[CT : 2 * CT, :], in_=ln2_b.rearrange("(r n) -> r n", r=CT))
         load_codes(wc[2][:], ffn2_w_words[4:6])
         load_codes(wc[3][:], ffn2_w_words[6:8])
         nc.sync.dma_start(out=s_bf[:], in_=scale_ffn.partition_broadcast(P))
         nc.sync.dma_start(out=sn_bf[:], in_=scale_norm2.partition_broadcast(P))
         load_h_codes(1)
         load_h_scales(1)
-        with nc.allow_non_contiguous_dma(reason="one channel to a partition, 1024 elements, once"):
-            nc.sync.dma_start(out=lnw_bf[:], in_=ln2_w.rearrange("(ct p) -> p ct", p=P))
-            nc.sync.dma_start(out=lnb_bf[:], in_=ln2_b.rearrange("(ct p) -> p ct", p=P))
         load_x(0)
         load_h_codes(2)
         load_h_scales(2)
@@ -197,17 +200,21 @@ def tile_transformerconvblock_pc_kernel(
             )
             nc.scalar.activation(out=st[tau][:, 4:5], in_=st[tau][:, 3:4], func=ACT.Sqrt, bias=one[:], scale=s2e[:])
 
-        def normalise(tau):
+        def normalise(tau, parts):
             nc.vector.reciprocal(out=st[tau][:, 5:6], in_=st[tau][:, 4:5])
-            t[tau] = t_pool.tile([P, CHANNELS], F32, name="t_t", tag="t_t")
-            nc.vector.tensor_scalar(
-                out=t[tau][:],
-                in0=y[tau][:],
-                scalar1=st[tau][:, 2:3],
-                scalar2=st[tau][:, 5:6],
-                op0=ALU.add,
-                op1=ALU.mult,
-            )
+            width = CHANNELS // parts
+            t[tau] = []
+            for k in range(parts):
+                part = t_pool.tile([P, width], F32, name="t_t", tag="t_t")
+                nc.vector.tensor_scalar(
+                    out=part[:],
+                    in0=y[tau][:, width * k : width * (k + 1)],
+                    scalar1=st[tau][:, 2:3],
+                    scalar2=st[tau][:, 5:6],
+                    op0=ALU.add,
+                    op1=ALU.mult,
+                )
+                t[tau].append(part)
 
         def transposes(i, halves):
             for k in range(4):
@@ -215,11 +222,15 @@ def tile_transformerconvblock_pc_kernel(
                 for j in range(2):
                     ct = 2 * k + j
                     for h in halves:
+                        parts = t[2 * i + h]
+                        per = CT // len(parts)
                         nc.tensor.transpose(
-                            tp[k][:, j, P * h : P * (h + 1)], t[2 * i + h][:, P * ct : P * (ct + 1)], ident[:]
+                            tp[k][:, j, P * h : P * (h + 1)],
+                            parts[ct // per][:, P * (ct % per) : P * (ct % per + 1)],
+                            ident[:],
                         )
 
-        def finish(i, halves):
+        def finish(i, halves, stores):
             cols = slice(P * halves[0], P * (halves[-1] + 1))
             if halves[0] == 0:
                 o[i] = o_pool.tile([P, CT, IMG_PIX], F32, name="o_t", tag="o_t")
@@ -232,18 +243,26 @@ def tile_transformerconvblock_pc_kernel(
                     op0=ALU.mult,
                     op1=ALU.add,
                 )
-            for ct in range(CT):
-                nc.scalar.activation(
-                    out=o[i][:, ct, cols], in_=o[i][:, ct, cols], func=ACT.Relu, bias=bv[:, ct : ct + 1], scale=1.0
+            per = CT // stores
+            for k in range(stores):
+                for ct in range(per * k, per * (k + 1)):
+                    nc.scalar.activation(
+                        out=o[i][:, ct, cols], in_=o[i][:, ct, cols], func=ACT.Relu, bias=bv[:, ct : ct + 1], scale=1.0
+                    )
+                nc.sync.dma_start(
+                    out=out[i].rearrange("(ct p) h w -> p ct (h w)", p=P)[:, per * k : per * (k + 1), cols],
+                    in_=o[i][:, per * k : per * (k + 1), cols],
                 )
-            nc.sync.dma_start(
-                out=out[i].rearrange("(ct p) h w -> p ct (h w)", p=P)[:, :, cols], in_=o[i][:, :, cols]
-            )
 
+        idle_out = psum.tile([P, BANK], F32, name="tp3", tag="tp3")
+        for k in range(8):
+            nc.tensor.matmul(out=idle_out[:], lhsT=ones[:], rhs=idle_rhs[:], start=True, stop=True)
         open_acc(0)
         open_acc(1)
         for g in range(PASSES):
             if g == 5:
+                vt = psum.tile([P, 32], F32, name="tp2", tag="tp2")
+                nc.tensor.matmul(out=vt[:], lhsT=vrows[:], rhs=ident_bf[:], start=True, stop=True)
                 for n in range(2):
                     bb = psum.tile([P, BANK], F32, name="tp%d" % n, tag="tp%d" % n)
                     nc.tensor.matmul(
@@ -257,39 +276,39 @@ def tile_transformerconvblock_pc_kernel(
         deviation(0)
         add_bias(1)
         deviation(1)
-        normalise(0)
-        normalise(1)
+        normalise(0, 1)
+        normalise(1, 1)
         nc.vector.tensor_scalar(
-            out=wv[:], in0=lnw_bf[:], scalar1=ssn[:], scalar2=EPS**-0.5, op0=ALU.mult, op1=ALU.mult
+            out=wv[:], in0=vt[:, 0:CT], scalar1=ssn[:], scalar2=EPS**-0.5, op0=ALU.mult, op1=ALU.mult
         )
-        nc.vector.tensor_scalar_mul(out=bv[:], in0=lnb_bf[:], scalar1=sn_bf[:])
+        nc.vector.tensor_scalar_mul(out=bv[:], in0=vt[:, CT : 2 * CT], scalar1=sn_bf[:])
 
         for i in range(1, IMAGES - 1):
             mx(2 * i)
             add_bias(2 * i)
             deviation(2 * i)
-            normalise(2 * i)
+            normalise(2 * i, 1)
             mx(2 * i + 1)
             add_bias(2 * i + 1)
             deviation(2 * i + 1)
             transposes(i - 1, (0, 1))
-            finish(i - 1, (0, 1))
+            finish(i - 1, (0, 1), 1)
             if i + 3 < IMAGES:
                 load_x(i + 3)
-            normalise(2 * i + 1)
+            normalise(2 * i + 1, 1)
 
         last = IMAGES - 1
         mx(2 * last)
         add_bias(2 * last)
         deviation(2 * last)
         transposes(last - 1, (0, 1))
-        finish(last - 1, (0, 1))
-        normalise(2 * last)
+        finish(last - 1, (0, 1), 1)
+        normalise(2 * last, 1)
         mx(2 * last + 1)
         add_bias(2 * last + 1)
         deviation(2 * last + 1)
         transposes(last, (0,))
-        finish(last, (0,))
-        normalise(2 * last + 1)
+        finish(last, (0,), 1)
+        normalise(2 * last + 1, 2)
         transposes(last, (1,))
-        finish(last, (1,))
+        finish(last, (1,), 4)

@@ -31,13 +31,13 @@ def tile_transformerconvblock_pc_kernel(
 
     with ExitStack() as ctx:
         keep = ctx.enter_context(tc.tile_pool(name="keep", bufs=1))
-        x_pool = ctx.enter_context(tc.tile_pool(name="x_pool", bufs=4))
+        x_pool = ctx.enter_context(tc.tile_pool(name="x_pool", bufs=6))
         y_pool = ctx.enter_context(tc.tile_pool(name="y_pool", bufs=3))
         sq_pool = ctx.enter_context(tc.tile_pool(name="sq_pool", bufs=2))
         st_pool = ctx.enter_context(tc.tile_pool(name="st_pool", bufs=4))
-        t_pool = ctx.enter_context(tc.tile_pool(name="t_pool", bufs=4))
-        o_pool = ctx.enter_context(tc.tile_pool(name="o_pool", bufs=3))
-        psum = ctx.enter_context(tc.psum_pool(name="psum", bufs=1))
+        t_pool = ctx.enter_context(tc.tile_pool(name="t_pool", bufs=6))
+        o_pool = ctx.enter_context(tc.tile_pool(name="o_pool", bufs=4))
+        psum = ctx.enter_context(tc.psum_pool(name="psum", bufs=8))
         ctx.enter_context(tc.manual_schedule())
 
         hc = []
@@ -130,6 +130,8 @@ def tile_transformerconvblock_pc_kernel(
         load_h_codes(3)
         load_h_scales(3)
         load_x(3)
+        load_x(4)
+        load_x(5)
         load_h_codes(4)
         load_h_scales(4)
         load_h_codes(5)
@@ -149,8 +151,7 @@ def tile_transformerconvblock_pc_kernel(
 
         def open_acc(tau):
             for n in range(2):
-                bank = 2 * (tau % 2) + n
-                acc[(tau, n)] = psum.tile([P, BANK], F32, name="acc%d" % bank, tag="acc%d" % bank)
+                acc[(tau, n)] = psum.tile([P, BANK], F32, name="bank", tag="bank")
 
         def mx_pass(tau, n, g):
             ci, off = where[tau]
@@ -217,15 +218,16 @@ def tile_transformerconvblock_pc_kernel(
                 t[tau].append(part)
 
         def transposes(i, halves):
+            tp[i] = []
             for k in range(4):
-                tp[k] = psum.tile([P, 2, IMG_PIX], F32, name="tp%d" % k, tag="tp%d" % k)
+                tp[i].append(psum.tile([P, 2, IMG_PIX], F32, name="bank", tag="bank"))
                 for j in range(2):
                     ct = 2 * k + j
                     for h in halves:
                         parts = t[2 * i + h]
                         per = CT // len(parts)
                         nc.tensor.transpose(
-                            tp[k][:, j, P * h : P * (h + 1)],
+                            tp[i][k][:, j, P * h : P * (h + 1)],
                             parts[ct // per][:, P * (ct % per) : P * (ct % per + 1)],
                             ident[:],
                         )
@@ -237,7 +239,7 @@ def tile_transformerconvblock_pc_kernel(
             for ct in range(CT):
                 nc.vector.scalar_tensor_tensor(
                     out=o[i][:, ct, cols],
-                    in0=tp[ct // 2][:, ct % 2, cols],
+                    in0=tp[i][ct // 2][:, ct % 2, cols],
                     scalar=wv[:, ct : ct + 1],
                     in1=x_tiles[i][:, ct, cols],
                     op0=ALU.mult,
@@ -254,17 +256,17 @@ def tile_transformerconvblock_pc_kernel(
                     in_=o[i][:, per * k : per * (k + 1), cols],
                 )
 
-        idle_out = psum.tile([P, BANK], F32, name="tp3", tag="tp3")
+        idle_out = psum.tile([P, BANK], F32, name="bank", tag="bank")
         for k in range(8):
             nc.tensor.matmul(out=idle_out[:], lhsT=ones[:], rhs=idle_rhs[:], start=True, stop=True)
         open_acc(0)
         open_acc(1)
         for g in range(PASSES):
             if g == 5:
-                vt = psum.tile([P, 32], F32, name="tp2", tag="tp2")
+                vt = psum.tile([P, 32], F32, name="bank", tag="bank")
                 nc.tensor.matmul(out=vt[:], lhsT=vrows[:], rhs=ident_bf[:], start=True, stop=True)
                 for n in range(2):
-                    bb = psum.tile([P, BANK], F32, name="tp%d" % n, tag="tp%d" % n)
+                    bb = psum.tile([P, BANK], F32, name="bank", tag="bank")
                     nc.tensor.matmul(
                         out=bb[:], lhsT=ones[:], rhs=brow[:, BANK * n : BANK * (n + 1)], start=True, stop=True
                     )
@@ -283,19 +285,21 @@ def tile_transformerconvblock_pc_kernel(
         )
         nc.vector.tensor_scalar_mul(out=bv[:], in0=vt[:, CT : 2 * CT], scalar1=sn_bf[:])
 
-        for i in range(1, IMAGES - 1):
-            mx(2 * i)
-            add_bias(2 * i)
-            deviation(2 * i)
-            normalise(2 * i, 1)
-            mx(2 * i + 1)
-            add_bias(2 * i + 1)
-            deviation(2 * i + 1)
-            transposes(i - 1, (0, 1))
-            finish(i - 1, (0, 1), 1)
-            if i + 3 < IMAGES:
-                load_x(i + 3)
-            normalise(2 * i + 1, 1)
+        for j in range(7):
+            for tau in range(4 * j + 2, 4 * j + 6):
+                mx(tau)
+                add_bias(tau)
+                deviation(tau)
+                if tau < 4 * j + 5:
+                    normalise(tau, 1)
+            transposes(2 * j, (0, 1))
+            transposes(2 * j + 1, (0, 1))
+            finish(2 * j, (0, 1), 1)
+            finish(2 * j + 1, (0, 1), 1)
+            for i in (2 * j + 6, 2 * j + 7):
+                if i < IMAGES:
+                    load_x(i)
+            normalise(4 * j + 5, 1)
 
         last = IMAGES - 1
         mx(2 * last)

@@ -22,6 +22,7 @@ IMG_PIX = 256
 CT = CHANNELS // P
 EPS = 1e-5
 CHUNKS = ((0, 1), (1, 1), (2, 2), (4, 4), (8, 4), (12, 4))
+W_GROUPS = ((0, 2), (2, 2), (4, 2), (6, 2))
 
 
 def tile_transformerconvblock_pc_kernel(
@@ -40,16 +41,28 @@ def tile_transformerconvblock_pc_kernel(
         psum = ctx.enter_context(tc.psum_pool(name="psum", bufs=8))
         ctx.enter_context(tc.manual_schedule())
 
+        def pass_groups(groups, width, name):
+            tiles = []
+            at = {}
+            for k, (g0, n_g) in enumerate(groups):
+                tiles.append(keep.tile([P, n_g, width], U8, name="%s_%d" % (name, k), align_bytes=64))
+                for g in range(n_g):
+                    at[g0 + g] = (tiles[k], g)
+            return tiles, at
+
         hc = []
         hp = []
+        hp_at = []
         where = {}
         for ci, (first, count) in enumerate(CHUNKS):
             hc.append(keep.tile([P, PASSES, 2 * IMG_PIX * count], U8, name="hc%d" % ci, align_bytes=64))
-            hp.append(keep.tile([P, PASSES, IMG_PIX * count], U8, name="hp%d" % ci, align_bytes=64))
+            tiles, at = pass_groups(((0, PASSES),), IMG_PIX * count, "hp%d" % ci)
+            hp.append(tiles)
+            hp_at.append(at)
             for k in range(2 * count):
                 where[2 * first + k] = (ci, P * k)
-        wc = [keep.tile([P, 2, 2 * CHANNELS], U8, name="wc%d" % k, align_bytes=64) for k in range(4)]
-        wp = [keep.tile([P, 4, CHANNELS], U8, name="wp%d" % k, align_bytes=64) for k in range(2)]
+        wc, wc_at = pass_groups(W_GROUPS, 2 * CHANNELS, "wc")
+        wp, wp_at = pass_groups(W_GROUPS, CHANNELS, "wp")
 
         brow = keep.tile([P, CHANNELS], BF16, name="brow")
         ones = keep.tile([P, P], BF16, name="ones")
@@ -82,9 +95,20 @@ def tile_transformerconvblock_pc_kernel(
             first, count = CHUNKS[ci]
             load_codes(hc[ci][:], h_words[:, :, 2 * IMG_PIX * first : 2 * IMG_PIX * (first + count)])
 
-        def load_h_scales(ci):
+        def load_h_scales(ci, k):
             first, count = CHUNKS[ci]
-            load_scales(hp[ci], h_scales[:, :, IMG_PIX * first : IMG_PIX * (first + count)])
+            load_scales(hp[ci][k], h_scales[:, :, IMG_PIX * first : IMG_PIX * (first + count)])
+
+        def load_w_codes(k):
+            g0, n_g = W_GROUPS[k]
+            load_codes(wc[k][:], ffn2_w_words[g0 : g0 + n_g])
+
+        def load_w_scales(k):
+            g0, n_g = W_GROUPS[k]
+            load_scales(wp[k], ffn2_w_scales[g0 : g0 + n_g])
+
+        def zero(plane):
+            nc.vector.memset(plane[:].bitcast(I32), 0)
 
         x_tiles = {}
 
@@ -92,50 +116,54 @@ def tile_transformerconvblock_pc_kernel(
             x_tiles[i] = x_pool.tile([P, CT, IMG_PIX], BF16, name="x_t", tag="x_t")
             nc.sync.dma_start(out=x_tiles[i][:], in_=x[i].rearrange("(ct p) h w -> p ct (h w)", p=P))
 
-        nc.vector.memset(hp[0][:].bitcast(I32), 0)
-        nc.vector.memset(wp[0][:].bitcast(I32), 0)
+        zero(hp[0][0])
+        zero(wp[0])
         nc.vector.memset(ones[:], 1.0)
         nc.vector.memset(idle_rhs[:], 0.0)
-        nc.vector.memset(wp[1][:].bitcast(I32), 0)
+        zero(wp[1])
+        zero(wp[2])
+        zero(wp[3])
         nc.vector.memset(brow[:], 0.0)
         nc.vector.memset(vrows[:], 0.0)
         nc.vector.memset(one[:], 1.0)
         nc.vector.memset(cneg[:], -1.0 / CHANNELS)
         for ci in range(1, len(CHUNKS)):
-            nc.vector.memset(hp[ci][:].bitcast(I32), 0)
+            zero(hp[ci][0])
         make_identity(nc, ident[:])
         nc.vector.tensor_copy(out=ident_bf[:], in_=ident[:, 0:32])
-        nc.scalar.activation(out=warm[:], in_=one[:], func=ACT.Sqrt)
+        nc.scalar.activation(out=warm[:], in_=one[:], func=ACT.Abs_reciprocal_sqrt)
 
-        load_h_scales(0)
         load_h_codes(0)
-        load_codes(wc[0][:], ffn2_w_words[0:2])
-        load_scales(wp[0], ffn2_w_scales[0:4])
-        load_codes(wc[1][:], ffn2_w_words[2:4])
-        load_scales(wp[1], ffn2_w_scales[4:8])
+        load_w_codes(0)
+        load_h_scales(0, 0)
+        load_w_scales(0)
+        load_w_scales(1)
+        load_w_codes(1)
+        load_w_scales(2)
+        load_w_codes(2)
         nc.sync.dma_start(out=brow[0:1, :], in_=ffn2_b.rearrange("(o n) -> o n", o=1))
         nc.sync.dma_start(out=vrows[0:CT, :], in_=ln2_w.rearrange("(r n) -> r n", r=CT))
         nc.sync.dma_start(out=vrows[CT : 2 * CT, :], in_=ln2_b.rearrange("(r n) -> r n", r=CT))
-        load_codes(wc[2][:], ffn2_w_words[4:6])
-        load_codes(wc[3][:], ffn2_w_words[6:8])
+        load_w_scales(3)
+        load_w_codes(3)
         nc.sync.dma_start(out=s_bf[:], in_=scale_ffn.partition_broadcast(P))
         nc.sync.dma_start(out=sn_bf[:], in_=scale_norm2.partition_broadcast(P))
         load_h_codes(1)
-        load_h_scales(1)
+        load_h_scales(1, 0)
         load_x(0)
         load_h_codes(2)
-        load_h_scales(2)
+        load_h_scales(2, 0)
         load_x(1)
         load_x(2)
         load_h_codes(3)
-        load_h_scales(3)
+        load_h_scales(3, 0)
         load_x(3)
         load_x(4)
         load_x(5)
         load_h_codes(4)
-        load_h_scales(4)
+        load_h_scales(4, 0)
         load_h_codes(5)
-        load_h_scales(5)
+        load_h_scales(5, 0)
 
         nc.vector.scalar_tensor_tensor(
             out=s2e[:], in0=s_bf[:], scalar=1.0 / (CHANNELS * EPS), in1=s_bf[:], op0=ALU.mult, op1=ALU.mult
@@ -155,12 +183,15 @@ def tile_transformerconvblock_pc_kernel(
 
         def mx_pass(tau, n, g):
             ci, off = where[tau]
+            x_plane, xg = hp_at[ci][g]
+            w_codes, cg = wc_at[g]
+            w_plane, wg = wp_at[g]
             nc.tensor.matmul_mx(
                 out=acc[(tau, n)][:],
                 lhsT=hc[ci][:, g, 2 * off : 2 * off + 2 * P].bitcast(FP4X4),
-                lhsT_scale=hp[ci][:, g, off : off + P],
-                rhs=wc[g // 2][:, g % 2, 2 * BANK * n : 2 * BANK * (n + 1)].bitcast(FP4X4),
-                rhs_scale=wp[g // 4][:, g % 4, BANK * n : BANK * (n + 1)],
+                lhsT_scale=x_plane[:, xg, off : off + P],
+                rhs=w_codes[:, cg, 2 * BANK * n : 2 * BANK * (n + 1)].bitcast(FP4X4),
+                rhs_scale=w_plane[:, wg, BANK * n : BANK * (n + 1)],
                 start=(g == 0),
                 stop=(g == PASSES - 1),
             )
@@ -199,10 +230,11 @@ def tile_transformerconvblock_pc_kernel(
             nc.scalar.activation(
                 out=sq[:], in_=y[tau][:], func=ACT.Square, bias=st[tau][:, 2:3], scale=1.0, accum_out=st[tau][:, 3:4]
             )
-            nc.scalar.activation(out=st[tau][:, 4:5], in_=st[tau][:, 3:4], func=ACT.Sqrt, bias=one[:], scale=s2e[:])
+            nc.scalar.activation(
+                out=st[tau][:, 5:6], in_=st[tau][:, 3:4], func=ACT.Abs_reciprocal_sqrt, bias=one[:], scale=s2e[:]
+            )
 
         def normalise(tau, parts):
-            nc.vector.reciprocal(out=st[tau][:, 5:6], in_=st[tau][:, 4:5])
             width = CHANNELS // parts
             t[tau] = []
             for k in range(parts):
@@ -257,12 +289,12 @@ def tile_transformerconvblock_pc_kernel(
                 )
 
         idle_out = psum.tile([P, BANK], F32, name="bank", tag="bank")
-        for k in range(8):
+        for k in range(5):
             nc.tensor.matmul(out=idle_out[:], lhsT=ones[:], rhs=idle_rhs[:], start=True, stop=True)
         open_acc(0)
         open_acc(1)
         for g in range(PASSES):
-            if g == 5:
+            if g == 6:
                 vt = psum.tile([P, 32], F32, name="bank", tag="bank")
                 nc.tensor.matmul(out=vt[:], lhsT=vrows[:], rhs=ident_bf[:], start=True, stop=True)
                 for n in range(2):

@@ -23,6 +23,8 @@ CT = CHANNELS // P
 EPS = 1e-5
 CHUNKS = ((0, 1), (1, 1), (2, 2), (4, 4), (8, 4), (12, 4))
 W_GROUPS = ((0, 2), (2, 2), (4, 2), (6, 2))
+MOVED = (3, 6, 9, 12)
+BLK = 32
 
 
 def tile_transformerconvblock_pc_kernel(
@@ -32,12 +34,13 @@ def tile_transformerconvblock_pc_kernel(
 
     with ExitStack() as ctx:
         keep = ctx.enter_context(tc.tile_pool(name="keep", bufs=1))
-        x_pool = ctx.enter_context(tc.tile_pool(name="x_pool", bufs=6))
+        x_pool = ctx.enter_context(tc.tile_pool(name="x_pool", bufs=5))
+        xq_pool = ctx.enter_context(tc.tile_pool(name="xq_pool", bufs=4))
         y_pool = ctx.enter_context(tc.tile_pool(name="y_pool", bufs=3))
         sq_pool = ctx.enter_context(tc.tile_pool(name="sq_pool", bufs=2))
         st_pool = ctx.enter_context(tc.tile_pool(name="st_pool", bufs=4))
         t_pool = ctx.enter_context(tc.tile_pool(name="t_pool", bufs=6))
-        o_pool = ctx.enter_context(tc.tile_pool(name="o_pool", bufs=4))
+        o_pool = ctx.enter_context(tc.tile_pool(name="o_pool", bufs=3))
         psum = ctx.enter_context(tc.psum_pool(name="psum", bufs=8))
         ctx.enter_context(tc.manual_schedule())
 
@@ -67,6 +70,10 @@ def tile_transformerconvblock_pc_kernel(
         brow = keep.tile([P, CHANNELS], BF16, name="brow")
         ones = keep.tile([P, P], BF16, name="ones")
         b_bc = keep.tile([P, CHANNELS], F32, name="b_bc")
+        g_bc = keep.tile([P, CHANNELS], F32, name="g_bc")
+        beta_bc = keep.tile([P, CHANNELS], F32, name="beta_bc")
+        gsc = keep.tile([P, 1], F32, name="gsc")
+        sn_f = keep.tile([P, 1], F32, name="sn_f")
         ident = keep.tile([P, P], F32, name="ident")
         one = keep.tile([P, 1], F32, name="one")
         cneg = keep.tile([P, 1], F32, name="cneg")
@@ -116,6 +123,35 @@ def tile_transformerconvblock_pc_kernel(
             x_tiles[i] = x_pool.tile([P, CT, IMG_PIX], BF16, name="x_t", tag="x_t")
             nc.sync.dma_start(out=x_tiles[i][:], in_=x[i].rearrange("(ct p) h w -> p ct (h w)", p=P))
 
+        xq_tiles = {}
+
+        def quadrant_view(dram_image, tau, a):
+            first = P * (tau % 2) + BLK * a
+            return dram_image.rearrange("(b s) h w -> s b (h w)", s=BLK)[:, :, first : first + BLK]
+
+        def load_xq(tau):
+            xq_tiles[tau] = xq_pool.tile([P, CHANNELS], BF16, name="xq_t", tag="xq_t")
+            for a in range(4):
+                nc.sync.dma_start(
+                    out=xq_tiles[tau][BLK * a : BLK * (a + 1), :].rearrange("p (b r) -> p b r", r=BLK),
+                    in_=quadrant_view(x[tau // 2], tau, a),
+                )
+
+        x_order = [i for i in range(IMAGES) if i not in MOVED]
+        xq_order = [2 * i + h for i in MOVED for h in range(2)]
+
+        loaded = {"x": 0, "xq": 0}
+
+        def load_next_x():
+            if loaded["x"] < len(x_order):
+                load_x(x_order[loaded["x"]])
+                loaded["x"] += 1
+
+        def load_next_xq():
+            if loaded["xq"] < len(xq_order):
+                load_xq(xq_order[loaded["xq"]])
+                loaded["xq"] += 1
+
         zero(hp[0][0])
         zero(wp[0])
         nc.vector.memset(ones[:], 1.0)
@@ -148,18 +184,23 @@ def tile_transformerconvblock_pc_kernel(
         load_w_codes(3)
         nc.sync.dma_start(out=s_bf[:], in_=scale_ffn.partition_broadcast(P))
         nc.sync.dma_start(out=sn_bf[:], in_=scale_norm2.partition_broadcast(P))
+        nc.sync.dma_start(out=brow[1:2, :], in_=ln2_w.rearrange("(o n) -> o n", o=1))
+        nc.sync.dma_start(out=brow[2:3, :], in_=ln2_b.rearrange("(o n) -> o n", o=1))
         load_h_codes(1)
         load_h_scales(1, 0)
-        load_x(0)
+        load_next_x()
         load_h_codes(2)
         load_h_scales(2, 0)
-        load_x(1)
-        load_x(2)
+        load_next_x()
+        load_next_x()
         load_h_codes(3)
         load_h_scales(3, 0)
-        load_x(3)
-        load_x(4)
-        load_x(5)
+        load_next_xq()
+        load_next_xq()
+        load_next_x()
+        load_next_x()
+        load_next_xq()
+        load_next_xq()
         load_h_codes(4)
         load_h_scales(4, 0)
         load_h_codes(5)
@@ -169,6 +210,8 @@ def tile_transformerconvblock_pc_kernel(
             out=s2e[:], in0=s_bf[:], scalar=1.0 / (CHANNELS * EPS), in1=s_bf[:], op0=ALU.mult, op1=ALU.mult
         )
         nc.vector.tensor_tensor(out=ssn[:], in0=s_bf[:], in1=sn_bf[:], op=ALU.mult)
+        nc.vector.tensor_scalar_mul(out=gsc[:], in0=ssn[:], scalar1=EPS**-0.5)
+        nc.vector.tensor_copy(out=sn_f[:], in_=sn_bf[:])
 
         acc = {}
         y = {}
@@ -203,7 +246,7 @@ def tile_transformerconvblock_pc_kernel(
                     mx_pass(tau, n, g)
 
         def add_bias(tau):
-            y[tau] = y_pool.tile([P, CHANNELS], F32, name="y_t", tag="y_t")
+            y[tau] = y_pool.tile([P, CHANNELS], F32, name="y_t", tag="y_t", align_bytes=64)
             st[tau] = st_pool.tile([P, 8], F32, name="st_t", tag="st_t")
             for n in range(2):
                 cols = slice(BANK * n, BANK * (n + 1))
@@ -238,7 +281,7 @@ def tile_transformerconvblock_pc_kernel(
             width = CHANNELS // parts
             t[tau] = []
             for k in range(parts):
-                part = t_pool.tile([P, width], F32, name="t_t", tag="t_t")
+                part = t_pool.tile([P, width], F32, name="t_t", tag="t_t", align_bytes=64)
                 nc.vector.tensor_scalar(
                     out=part[:],
                     in0=y[tau][:, width * k : width * (k + 1)],
@@ -248,6 +291,51 @@ def tile_transformerconvblock_pc_kernel(
                     op1=ALU.mult,
                 )
                 t[tau].append(part)
+
+        def tables():
+            for row, table, factor in ((1, g_bc, gsc), (2, beta_bc, sn_f)):
+                for n in range(2):
+                    cols = slice(BANK * n, BANK * (n + 1))
+                    spread = psum.tile([P, BANK], F32, name="bank", tag="bank")
+                    nc.tensor.matmul(
+                        out=spread[:],
+                        lhsT=ident_bf[:, row : row + 1].to_broadcast([P, P]),
+                        rhs=brow[:, cols],
+                        start=True,
+                        stop=True,
+                    )
+                    nc.scalar.activation(out=table[:, cols], in_=spread[:], func=ACT.Copy, scale=factor[:])
+
+        def moved_chain(tau):
+            u = t_pool.tile([P, CHANNELS], F32, name="t_t", tag="t_t", align_bytes=64)
+            halves = (slice(0, BANK), slice(BANK, CHANNELS))
+            for cols in halves:
+                nc.vector.scalar_tensor_tensor(
+                    out=y[tau][:, cols], in0=y[tau][:, cols], scalar=st[tau][:, 2:3], in1=g_bc[:, cols],
+                    op0=ALU.add, op1=ALU.mult,
+                )
+            for cols in halves:
+                nc.vector.scalar_tensor_tensor(
+                    out=y[tau][:, cols], in0=y[tau][:, cols], scalar=st[tau][:, 5:6], in1=beta_bc[:, cols],
+                    op0=ALU.mult, op1=ALU.add,
+                )
+            for cols in halves:
+                nc.vector.transpose(out=u[:, cols], in_=y[tau][:, cols])
+            for cols in halves:
+                nc.vector.tensor_tensor(out=u[:, cols], in0=u[:, cols], in1=xq_tiles[tau][:, cols], op=ALU.add)
+            nc.scalar.activation(out=u[:], in_=u[:], func=ACT.Relu)
+            for a in range(4):
+                nc.sync.dma_start(
+                    out=quadrant_view(out[tau // 2], tau, a),
+                    in_=u[BLK * a : BLK * (a + 1), :].rearrange("p (b r) -> p b r", r=BLK),
+                )
+            load_next_xq()
+
+        def post(tau):
+            if tau // 2 in MOVED:
+                moved_chain(tau)
+            else:
+                normalise(tau, 1)
 
         def transposes(i, halves):
             tp[i] = []
@@ -300,7 +388,11 @@ def tile_transformerconvblock_pc_kernel(
                 for n in range(2):
                     bb = psum.tile([P, BANK], F32, name="bank", tag="bank")
                     nc.tensor.matmul(
-                        out=bb[:], lhsT=ones[:], rhs=brow[:, BANK * n : BANK * (n + 1)], start=True, stop=True
+                        out=bb[:],
+                        lhsT=ident_bf[:, 0:1].to_broadcast([P, P]),
+                        rhs=brow[:, BANK * n : BANK * (n + 1)],
+                        start=True,
+                        stop=True,
                     )
                     nc.scalar.copy(out=b_bc[:, BANK * n : BANK * (n + 1)], in_=bb[:])
             for tau in range(2):
@@ -323,15 +415,17 @@ def tile_transformerconvblock_pc_kernel(
                 add_bias(tau)
                 deviation(tau)
                 if tau < 4 * j + 5:
-                    normalise(tau, 1)
-            transposes(2 * j, (0, 1))
-            transposes(2 * j + 1, (0, 1))
-            finish(2 * j, (0, 1), 1)
-            finish(2 * j + 1, (0, 1), 1)
-            for i in (2 * j + 6, 2 * j + 7):
-                if i < IMAGES:
-                    load_x(i)
-            normalise(4 * j + 5, 1)
+                    post(tau)
+                if tau == 3:
+                    tables()
+            turned = [i for i in (2 * j, 2 * j + 1) if i not in MOVED]
+            for i in turned:
+                transposes(i, (0, 1))
+            for i in turned:
+                finish(i, (0, 1), 1)
+            for i in turned:
+                load_next_x()
+            post(4 * j + 5)
 
         last = IMAGES - 1
         mx(2 * last)

@@ -25,6 +25,7 @@ CHUNKS = ((0, 1), (1, 1), (2, 2), (4, 4), (8, 4), (12, 4))
 W_GROUPS = ((0, 2), (2, 2), (4, 2), (6, 2))
 MOVED = (3, 6, 9, 12)
 BLK = 32
+PIECES = 3
 
 
 def tile_transformerconvblock_pc_kernel(
@@ -296,7 +297,7 @@ def tile_transformerconvblock_pc_kernel(
             for row, table, factor in ((1, g_bc, gsc), (2, beta_bc, sn_f)):
                 for n in range(2):
                     cols = slice(BANK * n, BANK * (n + 1))
-                    spread = psum.tile([P, BANK], F32, name="bank", tag="bank")
+                    spread, spread_rec = bank([P, BANK])
                     nc.tensor.matmul(
                         out=spread[:],
                         lhsT=ident_bf[:, row : row + 1].to_broadcast([P, P]),
@@ -305,37 +306,7 @@ def tile_transformerconvblock_pc_kernel(
                         stop=True,
                     )
                     nc.scalar.activation(out=table[:, cols], in_=spread[:], func=ACT.Copy, scale=factor[:])
-
-        def moved_chain(tau):
-            u = t_pool.tile([P, CHANNELS], F32, name="t_t", tag="t_t", align_bytes=64)
-            halves = (slice(0, BANK), slice(BANK, CHANNELS))
-            for cols in halves:
-                nc.vector.scalar_tensor_tensor(
-                    out=y[tau][:, cols], in0=y[tau][:, cols], scalar=st[tau][:, 2:3], in1=g_bc[:, cols],
-                    op0=ALU.add, op1=ALU.mult,
-                )
-            for cols in halves:
-                nc.vector.scalar_tensor_tensor(
-                    out=y[tau][:, cols], in0=y[tau][:, cols], scalar=st[tau][:, 5:6], in1=beta_bc[:, cols],
-                    op0=ALU.mult, op1=ALU.add,
-                )
-            for cols in halves:
-                nc.vector.transpose(out=u[:, cols], in_=y[tau][:, cols])
-            for cols in halves:
-                nc.vector.tensor_tensor(out=u[:, cols], in0=u[:, cols], in1=xq_tiles[tau][:, cols], op=ALU.add)
-            nc.scalar.activation(out=u[:], in_=u[:], func=ACT.Relu)
-            for a in range(4):
-                nc.sync.dma_start(
-                    out=quadrant_view(out[tau // 2], tau, a),
-                    in_=u[BLK * a : BLK * (a + 1), :].rearrange("p (b r) -> p b r", r=BLK),
-                )
-            load_next_xq()
-
-        def post(tau):
-            if tau // 2 in MOVED:
-                moved_chain(tau)
-            else:
-                normalise(tau, 1)
+                    spread_rec["done"] = True
 
         def transposes(i, halves):
             tp[i] = []
@@ -409,36 +380,230 @@ def tile_transformerconvblock_pc_kernel(
         )
         nc.vector.tensor_scalar_mul(out=bv[:], in0=vt[:, CT : 2 * CT], scalar1=sn_bf[:])
 
-        for j in range(7):
-            for tau in range(4 * j + 2, 4 * j + 6):
-                mx(tau)
-                add_bias(tau)
-                deviation(tau)
-                if tau < 4 * j + 5:
-                    post(tau)
-                if tau == 3:
-                    tables()
-            turned = [i for i in (2 * j, 2 * j + 1) if i not in MOVED]
-            for i in turned:
-                transposes(i, (0, 1))
-            for i in turned:
-                finish(i, (0, 1), 1)
-            for i in turned:
+        ring = [{"done": True} for k in range(8)]
+        todo = []
+        slow = []
+        late = []
+        at = {"todo": 0, "slow": 0, "drain": 0}
+
+        def pending():
+            return at["todo"] < len(todo) or at["slow"] < len(slow)
+
+        def drain_one():
+            assert pending()
+            if at["todo"] < len(todo):
+                at["todo"] += 1
+                todo[at["todo"] - 1]()
+            else:
+                at["slow"] += 1
+                slow[at["slow"] - 1]()
+
+        def drain(pieces):
+            at["drain"] += 1
+            for when, piece in list(late):
+                if when <= at["drain"]:
+                    late.remove((when, piece))
+                    piece()
+            for k in range(pieces):
+                if pending():
+                    drain_one()
+
+        def flush_late():
+            for when, piece in list(late):
+                late.remove((when, piece))
+                piece()
+
+        def bank(shape):
+            before = ring[len(ring) - 8]
+            while not before["done"]:
+                drain_one()
+            ring.append({"done": False})
+            return psum.tile(shape, F32, name="bank", tag="bank"), ring[len(ring) - 1]
+
+        recs = {}
+        normalised = {}
+
+        y_read = {}
+
+        def open_tile(tau):
+            for n in range(2):
+                acc[(tau, n)], recs[(tau, n)] = bank([P, BANK])
+            while tau >= 5 and not y_read.get(tau - 3, False):
+                drain_one()
+            y[tau] = y_pool.tile([P, CHANNELS], F32, name="y_t", tag="y_t", align_bytes=64)
+            st[tau] = st_pool.tile([P, 8], F32, name="st_t", tag="st_t")
+
+        def need_normalised(images):
+            for i in images:
+                for h in range(2):
+                    while not normalised.get(2 * i + h, False):
+                        drain_one()
+
+        def mx_tile(tau):
+            open_tile(tau)
+            for n in range(2):
+                for g in range(PASSES):
+                    mx_pass(tau, n, g)
+                bias_bank(tau, n)
+                recs[(tau, n)]["done"] = True
+                if n == 1:
+                    mean(tau)
+                    deviation(tau)
+                    if tau in runs:
+                        need_normalised(runs[tau])
+                        turn_images(runs[tau])
+                drain(PIECES)
+            queue_post(tau)
+
+        def bias_bank(tau, n):
+            cols = slice(BANK * n, BANK * (n + 1))
+            nc.vector.scalar_tensor_tensor(
+                out=y[tau][:, cols],
+                in0=acc[(tau, n)][:],
+                scalar=1.0,
+                in1=b_bc[:, cols],
+                op0=ALU.mult,
+                op1=ALU.add,
+                accum_out=st[tau][:, n : n + 1],
+            )
+
+        def mean(tau):
+            nc.vector.scalar_tensor_tensor(
+                out=st[tau][:, 2:3],
+                in0=st[tau][:, 0:1],
+                scalar=st[tau][:, 1:2],
+                in1=cneg[:],
+                op0=ALU.add,
+                op1=ALU.mult,
+            )
+
+        def queue_post(tau):
+            if tau // 2 in MOVED:
+                queue_moved(tau)
+            else:
+                todo.append(lambda: normalise_piece(tau))
+
+        def normalise_piece(tau):
+            normalise(tau, 1)
+            normalised[tau] = True
+            y_read[tau] = True
+
+        def queue_moved(tau):
+            halves = (slice(0, BANK), slice(BANK, CHANNELS))
+            u = {}
+
+            def gain(cols):
+                nc.vector.scalar_tensor_tensor(
+                    out=y[tau][:, cols], in0=y[tau][:, cols], scalar=st[tau][:, 2:3], in1=g_bc[:, cols],
+                    op0=ALU.add, op1=ALU.mult,
+                )
+
+            def shift(cols):
+                nc.vector.scalar_tensor_tensor(
+                    out=y[tau][:, cols], in0=y[tau][:, cols], scalar=st[tau][:, 5:6], in1=beta_bc[:, cols],
+                    op0=ALU.mult, op1=ALU.add,
+                )
+
+            def turn(cols):
+                if cols.start == 0:
+                    u[0] = t_pool.tile([P, CHANNELS], F32, name="t_t", tag="t_t", align_bytes=64)
+                nc.vector.transpose(out=u[0][:, cols], in_=y[tau][:, cols])
+                nc.gpsimd.tensor_tensor(out=u[0][:, cols], in0=u[0][:, cols], in1=xq_tiles[tau][:, cols], op=ALU.add)
+                if cols.start != 0:
+                    y_read[tau] = True
+                    late.append((at["drain"] + 2, leave))
+
+            def leave():
+                nc.scalar.activation(out=u[0][:], in_=u[0][:], func=ACT.Relu)
+                for a in range(4):
+                    nc.sync.dma_start(
+                        out=quadrant_view(out[tau // 2], tau, a),
+                        in_=u[0][BLK * a : BLK * (a + 1), :].rearrange("p (b r) -> p b r", r=BLK),
+                    )
+                load_next_xq()
+
+            for step in (gain, shift, turn):
+                for cols in halves:
+                    slow.append(lambda step=step, cols=cols: step(cols))
+
+        def turn_images(images):
+            for i in images:
+                tp[i] = []
+                tp_recs = []
+                for k in range(4):
+                    tile_k, rec_k = bank([P, 2, IMG_PIX])
+                    tp[i].append(tile_k)
+                    tp_recs.append(rec_k)
+                    for j in range(2):
+                        ct = 2 * k + j
+                        for h in range(2):
+                            nc.tensor.transpose(
+                                tp[i][k][:, j, P * h : P * (h + 1)], t[2 * i + h][0][:, P * ct : P * (ct + 1)], ident[:]
+                            )
+                for k in range(4):
+                    todo.append(lambda i=i, k=k, rec=tp_recs[k]: finish_bank(i, k, rec))
+
+        def finish_bank(i, k, rec):
+            if k == 0:
+                o[i] = o_pool.tile([P, CT, IMG_PIX], F32, name="o_t", tag="o_t")
+            for ct in (2 * k, 2 * k + 1):
+                nc.vector.scalar_tensor_tensor(
+                    out=o[i][:, ct, :],
+                    in0=tp[i][k][:, ct % 2, :],
+                    scalar=wv[:, ct : ct + 1],
+                    in1=x_tiles[i][:, ct, :],
+                    op0=ALU.mult,
+                    op1=ALU.add,
+                )
+            rec["done"] = True
+            for ct in (2 * k, 2 * k + 1):
+                nc.scalar.activation(
+                    out=o[i][:, ct, :], in_=o[i][:, ct, :], func=ACT.Relu, bias=bv[:, ct : ct + 1], scale=1.0
+                )
+            if k == 3:
+                nc.sync.dma_start(out=out[i].rearrange("(ct p) h w -> p ct (h w)", p=P), in_=o[i][:])
                 load_next_x()
-            post(4 * j + 5)
+
+        runs = {}
+        for i in range(IMAGES - 2):
+            if i not in MOVED:
+                runs[2 * i + 3] = (i,)
 
         last = IMAGES - 1
-        mx(2 * last)
-        add_bias(2 * last)
-        deviation(2 * last)
-        transposes(last - 1, (0, 1))
-        finish(last - 1, (0, 1), 1)
-        normalise(2 * last, 1)
-        mx(2 * last + 1)
-        add_bias(2 * last + 1)
-        deviation(2 * last + 1)
+        normalised[0] = True
+        normalised[1] = True
+        for tau in range(2, 2 * last):
+            mx_tile(tau)
+            if tau == 3:
+                tables()
+
+        tau = 2 * last
+        open_tile(tau)
+        for n in range(2):
+            for g in range(PASSES):
+                mx_pass(tau, n, g)
+            bias_bank(tau, n)
+            recs[(tau, n)]["done"] = True
+            if n == 0:
+                drain(PIECES)
+        mean(tau)
+        deviation(tau)
+        need_normalised((last - 1,))
+        turn_images((last - 1,))
+        while pending():
+            drain_one()
+        flush_late()
+        normalise(tau, 1)
+        tau = 2 * last + 1
+        open_tile(tau)
+        for n in range(2):
+            for g in range(PASSES):
+                mx_pass(tau, n, g)
+            bias_bank(tau, n)
+        mean(tau)
+        deviation(tau)
         transposes(last, (0,))
         finish(last, (0,), 1)
-        normalise(2 * last + 1, 2)
+        normalise(tau, 2)
         transposes(last, (1,))
         finish(last, (1,), 4)

@@ -23,8 +23,9 @@ CT = CHANNELS // P
 EPS = 1e-5
 CHUNKS = ((0, 1), (1, 1), (2, 2), (4, 4), (8, 4), (12, 4))
 W_GROUPS = ((0, 2), (2, 2), (4, 2), (6, 2))
-MOVED = (3, 6, 9, 12)
+MOVED = (2, 5, 8, 11)
 BLK = 32
+AGAIN = (5, 3)
 PIECES = 3
 
 
@@ -35,13 +36,14 @@ def tile_transformerconvblock_pc_kernel(
 
     with ExitStack() as ctx:
         keep = ctx.enter_context(tc.tile_pool(name="keep", bufs=1))
-        x_pool = ctx.enter_context(tc.tile_pool(name="x_pool", bufs=5))
+        x_pool = ctx.enter_context(tc.tile_pool(name="x_pool", bufs=6))
         xq_pool = ctx.enter_context(tc.tile_pool(name="xq_pool", bufs=4))
-        y_pool = ctx.enter_context(tc.tile_pool(name="y_pool", bufs=3))
+        y_pool = ctx.enter_context(tc.tile_pool(name="y_pool", bufs=4))
         sq_pool = ctx.enter_context(tc.tile_pool(name="sq_pool", bufs=2))
         st_pool = ctx.enter_context(tc.tile_pool(name="st_pool", bufs=4))
         t_pool = ctx.enter_context(tc.tile_pool(name="t_pool", bufs=6))
-        o_pool = ctx.enter_context(tc.tile_pool(name="o_pool", bufs=3))
+        o_pool = ctx.enter_context(tc.tile_pool(name="o_pool", bufs=4))
+        u_pool = ctx.enter_context(tc.tile_pool(name="u_pool", bufs=3))
         psum = ctx.enter_context(tc.psum_pool(name="psum", bufs=8))
         ctx.enter_context(tc.manual_schedule())
 
@@ -59,16 +61,22 @@ def tile_transformerconvblock_pc_kernel(
         hp_at = []
         where = {}
         for ci, (first, count) in enumerate(CHUNKS):
-            hc.append(keep.tile([P, PASSES, 2 * IMG_PIX * count], U8, name="hc%d" % ci, align_bytes=64))
-            tiles, at = pass_groups(((0, PASSES),), IMG_PIX * count, "hp%d" % ci)
-            hp.append(tiles)
-            hp_at.append(at)
+            if ci == AGAIN[0]:
+                hc.append(hc[AGAIN[1]])
+                hp.append(hp[AGAIN[1]])
+                hp_at.append(hp_at[AGAIN[1]])
+            else:
+                hc.append(keep.tile([P, PASSES, 2 * IMG_PIX * count], U8, name="hc%d" % ci, align_bytes=64))
+                tiles, at = pass_groups(((0, PASSES),), IMG_PIX * count, "hp%d" % ci)
+                hp.append(tiles)
+                hp_at.append(at)
             for k in range(2 * count):
                 where[2 * first + k] = (ci, P * k)
         wc, wc_at = pass_groups(W_GROUPS, 2 * CHANNELS, "wc")
         wp, wp_at = pass_groups(W_GROUPS, CHANNELS, "wp")
 
         brow = keep.tile([P, CHANNELS], BF16, name="brow")
+        lrow = keep.tile([P, CHANNELS], BF16, name="lrow")
         ones = keep.tile([P, P], BF16, name="ones")
         b_bc = keep.tile([P, CHANNELS], F32, name="b_bc")
         g_bc = keep.tile([P, CHANNELS], F32, name="g_bc")
@@ -162,10 +170,12 @@ def tile_transformerconvblock_pc_kernel(
         zero(wp[3])
         nc.vector.memset(brow[:], 0.0)
         nc.vector.memset(vrows[:], 0.0)
+        nc.vector.memset(lrow[:], 0.0)
         nc.vector.memset(one[:], 1.0)
         nc.vector.memset(cneg[:], -1.0 / CHANNELS)
         for ci in range(1, len(CHUNKS)):
-            zero(hp[ci][0])
+            if ci != AGAIN[0]:
+                zero(hp[ci][0])
         make_identity(nc, ident[:])
         nc.vector.tensor_copy(out=ident_bf[:], in_=ident[:, 0:32])
         nc.scalar.activation(out=warm[:], in_=one[:], func=ACT.Abs_reciprocal_sqrt)
@@ -185,8 +195,8 @@ def tile_transformerconvblock_pc_kernel(
         load_w_codes(3)
         nc.sync.dma_start(out=s_bf[:], in_=scale_ffn.partition_broadcast(P))
         nc.sync.dma_start(out=sn_bf[:], in_=scale_norm2.partition_broadcast(P))
-        nc.sync.dma_start(out=brow[1:2, :], in_=ln2_w.rearrange("(o n) -> o n", o=1))
-        nc.sync.dma_start(out=brow[2:3, :], in_=ln2_b.rearrange("(o n) -> o n", o=1))
+        nc.sync.dma_start(out=lrow[1:2, :], in_=ln2_w.rearrange("(o n) -> o n", o=1))
+        nc.sync.dma_start(out=lrow[2:3, :], in_=ln2_b.rearrange("(o n) -> o n", o=1))
         load_h_codes(1)
         load_h_scales(1, 0)
         load_next_x()
@@ -202,10 +212,9 @@ def tile_transformerconvblock_pc_kernel(
         load_next_x()
         load_next_xq()
         load_next_xq()
+        load_next_x()
         load_h_codes(4)
         load_h_scales(4, 0)
-        load_h_codes(5)
-        load_h_scales(5, 0)
 
         nc.vector.scalar_tensor_tensor(
             out=s2e[:], in0=s_bf[:], scalar=1.0 / (CHANNELS * EPS), in1=s_bf[:], op0=ALU.mult, op1=ALU.mult
@@ -301,7 +310,7 @@ def tile_transformerconvblock_pc_kernel(
                     nc.tensor.matmul(
                         out=spread[:],
                         lhsT=ident_bf[:, row : row + 1].to_broadcast([P, P]),
-                        rhs=brow[:, cols],
+                        rhs=lrow[:, cols],
                         start=True,
                         stop=True,
                     )
@@ -360,7 +369,7 @@ def tile_transformerconvblock_pc_kernel(
                     bb = psum.tile([P, BANK], F32, name="bank", tag="bank")
                     nc.tensor.matmul(
                         out=bb[:],
-                        lhsT=ident_bf[:, 0:1].to_broadcast([P, P]),
+                        lhsT=ones[:],
                         rhs=brow[:, BANK * n : BANK * (n + 1)],
                         start=True,
                         stop=True,
@@ -428,7 +437,7 @@ def tile_transformerconvblock_pc_kernel(
         def open_tile(tau):
             for n in range(2):
                 acc[(tau, n)], recs[(tau, n)] = bank([P, BANK])
-            while tau >= 5 and not y_read.get(tau - 3, False):
+            while tau >= 6 and not y_read.get(tau - 4, False):
                 drain_one()
             y[tau] = y_pool.tile([P, CHANNELS], F32, name="y_t", tag="y_t", align_bytes=64)
             st[tau] = st_pool.tile([P, 8], F32, name="st_t", tag="st_t")
@@ -449,6 +458,8 @@ def tile_transformerconvblock_pc_kernel(
                 if n == 1:
                     mean(tau)
                     deviation(tau)
+                    if tau // 2 not in MOVED and tau < 2 * (IMAGES - 2):
+                        normalise_on_scalar(tau)
                     if tau in runs:
                         need_normalised(runs[tau])
                         turn_images(runs[tau])
@@ -480,8 +491,18 @@ def tile_transformerconvblock_pc_kernel(
         def queue_post(tau):
             if tau // 2 in MOVED:
                 queue_moved(tau)
-            else:
+            elif tau >= 2 * (IMAGES - 2):
                 todo.append(lambda: normalise_piece(tau))
+
+        def normalise_on_scalar(tau):
+            nc.scalar.activation(out=st[tau][:, 6:7], in_=st[tau][:, 2:3], func=ACT.Copy, scale=st[tau][:, 5:6])
+            part = t_pool.tile([P, CHANNELS], F32, name="t_t", tag="t_t", align_bytes=64)
+            nc.scalar.activation(
+                out=part[:], in_=y[tau][:], func=ACT.Identity, bias=st[tau][:, 6:7], scale=st[tau][:, 5:6]
+            )
+            t[tau] = [part]
+            normalised[tau] = True
+            y_read[tau] = True
 
         def normalise_piece(tau):
             normalise(tau, 1)
@@ -506,12 +527,15 @@ def tile_transformerconvblock_pc_kernel(
 
             def turn(cols):
                 if cols.start == 0:
-                    u[0] = t_pool.tile([P, CHANNELS], F32, name="t_t", tag="t_t", align_bytes=64)
+                    u[0] = u_pool.tile([P, CHANNELS], F32, name="u_t", tag="u_t", align_bytes=64)
                 nc.vector.transpose(out=u[0][:, cols], in_=y[tau][:, cols])
-                nc.gpsimd.tensor_tensor(out=u[0][:, cols], in0=u[0][:, cols], in1=xq_tiles[tau][:, cols], op=ALU.add)
                 if cols.start != 0:
                     y_read[tau] = True
-                    late.append((at["drain"] + 2, leave))
+
+            def add_x(cols):
+                nc.vector.tensor_tensor(out=u[0][:, cols], in0=u[0][:, cols], in1=xq_tiles[tau][:, cols], op=ALU.add)
+                if cols.start != 0:
+                    late.append((at["drain"] + 1, leave))
 
             def leave():
                 nc.scalar.activation(out=u[0][:], in_=u[0][:], func=ACT.Relu)
@@ -522,7 +546,7 @@ def tile_transformerconvblock_pc_kernel(
                     )
                 load_next_xq()
 
-            for step in (gain, shift, turn):
+            for step in (gain, shift, turn, add_x):
                 for cols in halves:
                     slow.append(lambda step=step, cols=cols: step(cols))
 
@@ -576,6 +600,9 @@ def tile_transformerconvblock_pc_kernel(
             mx_tile(tau)
             if tau == 3:
                 tables()
+            if tau == 2 * (CHUNKS[AGAIN[1]][0] + CHUNKS[AGAIN[1]][1]) - 1:
+                load_h_scales(AGAIN[0], 0)
+                load_h_codes(AGAIN[0])
 
         tau = 2 * last
         open_tile(tau)

@@ -76,12 +76,11 @@ def tile_transformerconvblock_pc_kernel(
         wp, wp_at = pass_groups(W_GROUPS, CHANNELS, "wp")
 
         brow = keep.tile([P, CHANNELS], BF16, name="brow")
-        lrow = keep.tile([P, CHANNELS], BF16, name="lrow")
         ones = keep.tile([P, P], BF16, name="ones")
         b_bc = keep.tile([P, CHANNELS], F32, name="b_bc")
-        g_bc = keep.tile([P, CHANNELS], F32, name="g_bc")
-        beta_bc = keep.tile([P, CHANNELS], F32, name="beta_bc")
-        gsc = keep.tile([P, 1], F32, name="gsc")
+        lw_bc = keep.tile([P, CHANNELS], BF16, name="lw_bc")
+        lb_bc = keep.tile([P, CHANNELS], BF16, name="lb_bc")
+        s_eps = keep.tile([P, 1], F32, name="s_eps")
         sn_f = keep.tile([P, 1], F32, name="sn_f")
         ident = keep.tile([P, P], F32, name="ident")
         one = keep.tile([P, 1], F32, name="one")
@@ -170,7 +169,6 @@ def tile_transformerconvblock_pc_kernel(
         zero(wp[3])
         nc.vector.memset(brow[:], 0.0)
         nc.vector.memset(vrows[:], 0.0)
-        nc.vector.memset(lrow[:], 0.0)
         nc.vector.memset(one[:], 1.0)
         nc.vector.memset(cneg[:], -1.0 / CHANNELS)
         for ci in range(1, len(CHUNKS)):
@@ -195,8 +193,6 @@ def tile_transformerconvblock_pc_kernel(
         load_w_codes(3)
         nc.sync.dma_start(out=s_bf[:], in_=scale_ffn.partition_broadcast(P))
         nc.sync.dma_start(out=sn_bf[:], in_=scale_norm2.partition_broadcast(P))
-        nc.sync.dma_start(out=lrow[1:2, :], in_=ln2_w.rearrange("(o n) -> o n", o=1))
-        nc.sync.dma_start(out=lrow[2:3, :], in_=ln2_b.rearrange("(o n) -> o n", o=1))
         load_h_codes(1)
         load_h_scales(1, 0)
         load_next_x()
@@ -204,6 +200,8 @@ def tile_transformerconvblock_pc_kernel(
         load_h_scales(2, 0)
         load_next_x()
         load_next_x()
+        nc.sync.dma_start(out=lw_bc[:], in_=ln2_w.partition_broadcast(P))
+        nc.sync.dma_start(out=lb_bc[:], in_=ln2_b.partition_broadcast(P))
         load_h_codes(3)
         load_h_scales(3, 0)
         load_next_xq()
@@ -220,7 +218,7 @@ def tile_transformerconvblock_pc_kernel(
             out=s2e[:], in0=s_bf[:], scalar=1.0 / (CHANNELS * EPS), in1=s_bf[:], op0=ALU.mult, op1=ALU.mult
         )
         nc.vector.tensor_tensor(out=ssn[:], in0=s_bf[:], in1=sn_bf[:], op=ALU.mult)
-        nc.vector.tensor_scalar_mul(out=gsc[:], in0=ssn[:], scalar1=EPS**-0.5)
+        nc.vector.tensor_scalar_mul(out=s_eps[:], in0=s_bf[:], scalar1=EPS**-0.5)
         nc.vector.tensor_copy(out=sn_f[:], in_=sn_bf[:])
 
         acc = {}
@@ -301,21 +299,6 @@ def tile_transformerconvblock_pc_kernel(
                     op1=ALU.mult,
                 )
                 t[tau].append(part)
-
-        def tables():
-            for row, table, factor in ((1, g_bc, gsc), (2, beta_bc, sn_f)):
-                for n in range(2):
-                    cols = slice(BANK * n, BANK * (n + 1))
-                    spread, spread_rec = bank([P, BANK])
-                    nc.tensor.matmul(
-                        out=spread[:],
-                        lhsT=ident_bf[:, row : row + 1].to_broadcast([P, P]),
-                        rhs=lrow[:, cols],
-                        start=True,
-                        stop=True,
-                    )
-                    nc.scalar.activation(out=table[:, cols], in_=spread[:], func=ACT.Copy, scale=factor[:])
-                    spread_rec["done"] = True
 
         def transposes(i, halves):
             tp[i] = []
@@ -458,7 +441,11 @@ def tile_transformerconvblock_pc_kernel(
                 if n == 1:
                     mean(tau)
                     deviation(tau)
-                    if tau // 2 not in MOVED and tau < 2 * (IMAGES - 2):
+                    if tau // 2 in MOVED:
+                        nc.scalar.activation(
+                            out=st[tau][:, 6:7], in_=st[tau][:, 5:6], func=ACT.Copy, scale=s_eps[:]
+                        )
+                    elif tau < 2 * (IMAGES - 2):
                         normalise_on_scalar(tau)
                     if tau in runs:
                         need_normalised(runs[tau])
@@ -515,13 +502,13 @@ def tile_transformerconvblock_pc_kernel(
 
             def gain(cols):
                 nc.vector.scalar_tensor_tensor(
-                    out=y[tau][:, cols], in0=y[tau][:, cols], scalar=st[tau][:, 2:3], in1=g_bc[:, cols],
+                    out=y[tau][:, cols], in0=y[tau][:, cols], scalar=st[tau][:, 2:3], in1=lw_bc[:, cols],
                     op0=ALU.add, op1=ALU.mult,
                 )
 
             def shift(cols):
                 nc.vector.scalar_tensor_tensor(
-                    out=y[tau][:, cols], in0=y[tau][:, cols], scalar=st[tau][:, 5:6], in1=beta_bc[:, cols],
+                    out=y[tau][:, cols], in0=y[tau][:, cols], scalar=st[tau][:, 6:7], in1=lb_bc[:, cols],
                     op0=ALU.mult, op1=ALU.add,
                 )
 
@@ -533,7 +520,10 @@ def tile_transformerconvblock_pc_kernel(
                     y_read[tau] = True
 
             def add_x(cols):
-                nc.vector.tensor_tensor(out=u[0][:, cols], in0=u[0][:, cols], in1=xq_tiles[tau][:, cols], op=ALU.add)
+                nc.vector.scalar_tensor_tensor(
+                    out=u[0][:, cols], in0=u[0][:, cols], scalar=sn_f[:], in1=xq_tiles[tau][:, cols],
+                    op0=ALU.mult, op1=ALU.add,
+                )
                 if cols.start != 0:
                     late.append((at["drain"] + 1, leave))
 
@@ -598,8 +588,6 @@ def tile_transformerconvblock_pc_kernel(
         normalised[1] = True
         for tau in range(2, 2 * last):
             mx_tile(tau)
-            if tau == 3:
-                tables()
             if tau == 2 * (CHUNKS[AGAIN[1]][0] + CHUNKS[AGAIN[1]][1]) - 1:
                 load_h_scales(AGAIN[0], 0)
                 load_h_codes(AGAIN[0])

@@ -579,9 +579,15 @@ def tile_transformerconvblock_pc_kernel(
                 load_next_x()
 
         runs = {}
-        for i in range(IMAGES - 2):
-            if i not in MOVED:
-                runs[2 * i + 3] = (i,)
+        plain = [i for i in range(IMAGES - 2) if i not in MOVED]
+        k = 0
+        while k < len(plain):
+            if k + 1 < len(plain) and plain[k + 1] == plain[k] + 1 and plain[k + 1] < IMAGES - 4:
+                runs[2 * plain[k + 1] + 3] = (plain[k], plain[k + 1])
+                k += 2
+            else:
+                runs[2 * plain[k] + 3] = (plain[k],)
+                k += 1
 
         last = IMAGES - 1
         normalised[0] = True

@@ -86,6 +86,7 @@ def tile_transformerconvblock_pc_kernel(
         one = keep.tile([P, 1], F32, name="one")
         cneg = keep.tile([P, 1], F32, name="cneg")
         warm = keep.tile([P, 1], F32, name="warm")
+        two = keep.tile([P, 2], F32, name="two")
         s_bf = keep.tile([P, 1], BF16, name="s_bf")
         sn_bf = keep.tile([P, 1], BF16, name="sn_bf")
         s2e = keep.tile([P, 1], F32, name="s2e")
@@ -445,7 +446,7 @@ def tile_transformerconvblock_pc_kernel(
                         nc.scalar.activation(
                             out=st[tau][:, 6:7], in_=st[tau][:, 5:6], func=ACT.Copy, scale=s_eps[:]
                         )
-                    elif tau < 2 * (IMAGES - 2):
+                    elif tau < 2 * (IMAGES - 1):
                         normalise_on_scalar(tau)
                     if tau in runs:
                         need_normalised(runs[tau])
@@ -466,19 +467,14 @@ def tile_transformerconvblock_pc_kernel(
             )
 
         def mean(tau):
-            nc.vector.scalar_tensor_tensor(
-                out=st[tau][:, 2:3],
-                in0=st[tau][:, 0:1],
-                scalar=st[tau][:, 1:2],
-                in1=cneg[:],
-                op0=ALU.add,
-                op1=ALU.mult,
+            nc.scalar.activation(
+                out=two[:], in_=st[tau][:, 0:2], func=ACT.Copy, scale=-1.0 / CHANNELS, accum_out=st[tau][:, 2:3]
             )
 
         def queue_post(tau):
             if tau // 2 in MOVED:
                 queue_moved(tau)
-            elif tau >= 2 * (IMAGES - 2):
+            elif tau >= 2 * (IMAGES - 1):
                 todo.append(lambda: normalise_piece(tau))
 
         def normalise_on_scalar(tau):

@@ -75,9 +75,8 @@ def tile_transformerconvblock_pc_kernel(
         wc, wc_at = pass_groups(W_GROUPS, 2 * CHANNELS, "wc")
         wp, wp_at = pass_groups(W_GROUPS, CHANNELS, "wp")
 
-        brow = keep.tile([P, CHANNELS], BF16, name="brow")
         ones = keep.tile([P, P], BF16, name="ones")
-        b_bc = keep.tile([P, CHANNELS], F32, name="b_bc")
+        b_bc = keep.tile([P, CHANNELS], BF16, name="b_bc")
         lw_bc = keep.tile([P, CHANNELS], BF16, name="lw_bc")
         lb_bc = keep.tile([P, CHANNELS], BF16, name="lb_bc")
         s_eps = keep.tile([P, 1], F32, name="s_eps")
@@ -168,7 +167,6 @@ def tile_transformerconvblock_pc_kernel(
         zero(wp[1])
         zero(wp[2])
         zero(wp[3])
-        nc.vector.memset(brow[:], 0.0)
         nc.vector.memset(vrows[:], 0.0)
         nc.vector.memset(one[:], 1.0)
         nc.vector.memset(cneg[:], -1.0 / CHANNELS)
@@ -187,7 +185,7 @@ def tile_transformerconvblock_pc_kernel(
         load_w_codes(1)
         load_w_scales(2)
         load_w_codes(2)
-        nc.sync.dma_start(out=brow[0:1, :], in_=ffn2_b.rearrange("(o n) -> o n", o=1))
+        nc.sync.dma_start(out=b_bc[:], in_=ffn2_b.partition_broadcast(P))
         nc.sync.dma_start(out=vrows[0:CT, :], in_=ln2_w.rearrange("(r n) -> r n", r=CT))
         nc.sync.dma_start(out=vrows[CT : 2 * CT, :], in_=ln2_b.rearrange("(r n) -> r n", r=CT))
         load_w_scales(3)
@@ -349,16 +347,6 @@ def tile_transformerconvblock_pc_kernel(
             if g == 6:
                 vt = psum.tile([P, 32], F32, name="bank", tag="bank")
                 nc.tensor.matmul(out=vt[:], lhsT=vrows[:], rhs=ident_bf[:], start=True, stop=True)
-                for n in range(2):
-                    bb = psum.tile([P, BANK], F32, name="bank", tag="bank")
-                    nc.tensor.matmul(
-                        out=bb[:],
-                        lhsT=ones[:],
-                        rhs=brow[:, BANK * n : BANK * (n + 1)],
-                        start=True,
-                        stop=True,
-                    )
-                    nc.scalar.copy(out=b_bc[:, BANK * n : BANK * (n + 1)], in_=bb[:])
             for tau in range(2):
                 for n in range(2):
                     mx_pass(tau, n, g)

@@ -185,7 +185,6 @@ def tile_transformerconvblock_pc_kernel(
         load_w_codes(1)
         load_w_scales(2)
         load_w_codes(2)
-        nc.sync.dma_start(out=b_bc[:], in_=ffn2_b.partition_broadcast(P))
         nc.sync.dma_start(out=vrows[0:CT, :], in_=ln2_w.rearrange("(r n) -> r n", r=CT))
         nc.sync.dma_start(out=vrows[CT : 2 * CT, :], in_=ln2_b.rearrange("(r n) -> r n", r=CT))
         load_w_scales(3)
@@ -194,6 +193,7 @@ def tile_transformerconvblock_pc_kernel(
         nc.sync.dma_start(out=sn_bf[:], in_=scale_norm2.partition_broadcast(P))
         load_h_codes(1)
         load_h_scales(1, 0)
+        nc.sync.dma_start(out=b_bc[:], in_=ffn2_b.partition_broadcast(P))
         load_next_x()
         load_h_codes(2)
         load_h_scales(2, 0)

from contextlib import ExitStack

import concourse.mybir as mybir
from concourse.masks import make_identity

FLOPS = 2 * 4096 * 4096 * 1024

F32 = mybir.dt.float32
BF16 = mybir.dt.bfloat16
U8 = mybir.dt.uint8
I32 = mybir.dt.int32
FP4X4 = mybir.dt.float4_e2m1fn_x4
ALU = mybir.AluOpType
ACT = mybir.ActivationFunctionType

P = 128
PASSES = 8
CHANNELS = 1024
BANK = 512
IMAGES = 16
IMG_PIX = 256
CT = CHANNELS // P
EPS = 1e-5
CHUNKS = ((0, 1), (1, 1), (2, 2), (4, 4), (8, 4), (12, 4))
W_GROUPS = ((0, 2), (2, 2), (4, 2), (6, 2))
MOVED = (2, 5, 8, 11)
BLK = 32
AGAIN = (5, 3)
PIECES = 3


def tile_transformerconvblock_pc_kernel(
    tc, h_words, h_scales, ffn2_w_words, ffn2_w_scales, ffn2_b, scale_ffn, ln2_w, ln2_b, scale_norm2, x, out
):
    nc = tc.nc

    with ExitStack() as ctx:
        keep = ctx.enter_context(tc.tile_pool(name="keep", bufs=1))
        x_pool = ctx.enter_context(tc.tile_pool(name="x_pool", bufs=6))
        xq_pool = ctx.enter_context(tc.tile_pool(name="xq_pool", bufs=4))
        y_pool = ctx.enter_context(tc.tile_pool(name="y_pool", bufs=4))
        sq_pool = ctx.enter_context(tc.tile_pool(name="sq_pool", bufs=2))
        st_pool = ctx.enter_context(tc.tile_pool(name="st_pool", bufs=4))
        t_pool = ctx.enter_context(tc.tile_pool(name="t_pool", bufs=6))
        o_pool = ctx.enter_context(tc.tile_pool(name="o_pool", bufs=4))
        u_pool = ctx.enter_context(tc.tile_pool(name="u_pool", bufs=3))
        psum = ctx.enter_context(tc.psum_pool(name="psum", bufs=8))
        ctx.enter_context(tc.manual_schedule())

        def pass_groups(groups, width, name):
            tiles = []
            at = {}
            for k, (g0, n_g) in enumerate(groups):
                tiles.append(keep.tile([P, n_g, width], U8, name="%s_%d" % (name, k), align_bytes=64))
                for g in range(n_g):
                    at[g0 + g] = (tiles[k], g)
            return tiles, at

        hc = []
        hp = []
        hp_at = []
        where = {}
        for ci, (first, count) in enumerate(CHUNKS):
            if ci == AGAIN[0]:
                hc.append(hc[AGAIN[1]])
                hp.append(hp[AGAIN[1]])
                hp_at.append(hp_at[AGAIN[1]])
            else:
                hc.append(keep.tile([P, PASSES, 2 * IMG_PIX * count], U8, name="hc%d" % ci, align_bytes=64))
                tiles, at = pass_groups(((0, PASSES),), IMG_PIX * count, "hp%d" % ci)
                hp.append(tiles)
                hp_at.append(at)
            for k in range(2 * count):
                where[2 * first + k] = (ci, P * k)
        wc, wc_at = pass_groups(W_GROUPS, 2 * CHANNELS, "wc")
        wp, wp_at = pass_groups(W_GROUPS, CHANNELS, "wp")

        ones = keep.tile([P, P], BF16, name="ones")
        b_bc = keep.tile([P, CHANNELS], BF16, name="b_bc")
        lw_bc = keep.tile([P, CHANNELS], BF16, name="lw_bc")
        lb_bc = keep.tile([P, CHANNELS], BF16, name="lb_bc")
        s_eps = keep.tile([P, 1], F32, name="s_eps")
        sn_f = keep.tile([P, 1], F32, name="sn_f")
        ident = keep.tile([P, P], F32, name="ident")
        one = keep.tile([P, 1], F32, name="one")
        cneg = keep.tile([P, 1], F32, name="cneg")
        warm = keep.tile([P, 1], F32, name="warm")
        two = keep.tile([P, 2], F32, name="two")
        s_bf = keep.tile([P, 1], BF16, name="s_bf")
        sn_bf = keep.tile([P, 1], BF16, name="sn_bf")
        s2e = keep.tile([P, 1], F32, name="s2e")
        ssn = keep.tile([P, 1], F32, name="ssn")
        vrows = keep.tile([P, P], BF16, name="vrows")
        ident_bf = keep.tile([P, 32], BF16, name="ident_bf")
        idle_rhs = keep.tile([P, BANK], BF16, name="idle_rhs")
        wv = keep.tile([P, CT], F32, name="wv")
        bv = keep.tile([P, CT], F32, name="bv")

        def load_codes(dst, src):
            nc.sync.dma_start(out=dst.bitcast(I32), in_=src.rearrange("g p n -> p g n").bitcast(I32))

        def load_scales(dst, src):
            for q in range(4):
                nc.sync.dma_start(
                    out=dst[32 * q : 32 * q + 4, :, :].bitcast(I32),
                    in_=src[:, 4 * q : 4 * q + 4, :].rearrange("g r n -> r g n").bitcast(I32),
                )

        def load_h_codes(ci):
            first, count = CHUNKS[ci]
            load_codes(hc[ci][:], h_words[:, :, 2 * IMG_PIX * first : 2 * IMG_PIX * (first + count)])

        def load_h_scales(ci, k):
            first, count = CHUNKS[ci]
            load_scales(hp[ci][k], h_scales[:, :, IMG_PIX * first : IMG_PIX * (first + count)])

        def load_w_codes(k):
            g0, n_g = W_GROUPS[k]
            load_codes(wc[k][:], ffn2_w_words[g0 : g0 + n_g])

        def load_w_scales(k):
            g0, n_g = W_GROUPS[k]
            load_scales(wp[k], ffn2_w_scales[g0 : g0 + n_g])

        def zero(plane):
            nc.vector.memset(plane[:].bitcast(I32), 0)

        x_tiles = {}

        def load_x(i):
            x_tiles[i] = x_pool.tile([P, CT, IMG_PIX], BF16, name="x_t", tag="x_t")
            nc.sync.dma_start(out=x_tiles[i][:], in_=x[i].rearrange("(ct p) h w -> p ct (h w)", p=P))

        xq_tiles = {}

        def quadrant_view(dram_image, tau, a):
            first = P * (tau % 2) + BLK * a
            return dram_image.rearrange("(b s) h w -> s b (h w)", s=BLK)[:, :, first : first + BLK]

        def load_xq(tau):
            xq_tiles[tau] = xq_pool.tile([P, CHANNELS], BF16, name="xq_t", tag="xq_t")
            for a in range(4):
                nc.sync.dma_start(
                    out=xq_tiles[tau][BLK * a : BLK * (a + 1), :].rearrange("p (b r) -> p b r", r=BLK),
                    in_=quadrant_view(x[tau // 2], tau, a),
                )

        x_order = [i for i in range(IMAGES) if i not in MOVED]
        xq_order = [2 * i + h for i in MOVED for h in range(2)]

        loaded = {"x": 0, "xq": 0}

        def load_next_x():
            if loaded["x"] < len(x_order):
                load_x(x_order[loaded["x"]])
                loaded["x"] += 1

        def load_next_xq():
            if loaded["xq"] < len(xq_order):
                load_xq(xq_order[loaded["xq"]])
                loaded["xq"] += 1

        zero(hp[0][0])
        zero(wp[0])
        nc.vector.memset(ones[:], 1.0)
        nc.vector.memset(idle_rhs[:], 0.0)
        zero(wp[1])
        zero(wp[2])
        zero(wp[3])
        nc.vector.memset(vrows[:], 0.0)
        nc.vector.memset(one[:], 1.0)
        nc.vector.memset(cneg[:], -1.0 / CHANNELS)
        for ci in range(1, len(CHUNKS)):
            if ci != AGAIN[0]:
                zero(hp[ci][0])
        make_identity(nc, ident[:])
        nc.vector.tensor_copy(out=ident_bf[:], in_=ident[:, 0:32])
        nc.scalar.activation(out=warm[:], in_=one[:], func=ACT.Abs_reciprocal_sqrt)

        load_h_codes(0)
        load_w_codes(0)
        load_h_scales(0, 0)
        load_w_scales(0)
        load_w_scales(1)
        load_w_codes(1)
        load_w_scales(2)
        load_w_codes(2)
        nc.sync.dma_start(out=vrows[0:CT, :], in_=ln2_w.rearrange("(r n) -> r n", r=CT))
        nc.sync.dma_start(out=vrows[CT : 2 * CT, :], in_=ln2_b.rearrange("(r n) -> r n", r=CT))
        load_w_scales(3)
        load_w_codes(3)
        nc.sync.dma_start(out=s_bf[:], in_=scale_ffn.partition_broadcast(P))
        nc.sync.dma_start(out=sn_bf[:], in_=scale_norm2.partition_broadcast(P))
        load_h_codes(1)
        load_h_scales(1, 0)
        nc.sync.dma_start(out=b_bc[:], in_=ffn2_b.partition_broadcast(P))
        load_next_x()
        load_h_codes(2)
        load_h_scales(2, 0)
        load_next_x()
        load_next_x()
        nc.sync.dma_start(out=lw_bc[:], in_=ln2_w.partition_broadcast(P))
        nc.sync.dma_start(out=lb_bc[:], in_=ln2_b.partition_broadcast(P))
        load_h_codes(3)
        load_h_scales(3, 0)
        load_next_xq()
        load_next_xq()
        load_next_x()
        load_next_x()
        load_next_xq()
        load_next_xq()
        load_next_x()
        load_h_codes(4)
        load_h_scales(4, 0)

        nc.vector.scalar_tensor_tensor(
            out=s2e[:], in0=s_bf[:], scalar=1.0 / (CHANNELS * EPS), in1=s_bf[:], op0=ALU.mult, op1=ALU.mult
        )
        nc.vector.tensor_tensor(out=ssn[:], in0=s_bf[:], in1=sn_bf[:], op=ALU.mult)
        nc.vector.tensor_scalar_mul(out=s_eps[:], in0=s_bf[:], scalar1=EPS**-0.5)
        nc.vector.tensor_copy(out=sn_f[:], in_=sn_bf[:])

        acc = {}
        y = {}
        st = {}
        t = {}
        tp = {}
        o = {}

        def open_acc(tau):
            for n in range(2):
                acc[(tau, n)] = psum.tile([P, BANK], F32, name="bank", tag="bank")

        def mx_pass(tau, n, g):
            ci, off = where[tau]
            x_plane, xg = hp_at[ci][g]
            w_codes, cg = wc_at[g]
            w_plane, wg = wp_at[g]
            nc.tensor.matmul_mx(
                out=acc[(tau, n)][:],
                lhsT=hc[ci][:, g, 2 * off : 2 * off + 2 * P].bitcast(FP4X4),
                lhsT_scale=x_plane[:, xg, off : off + P],
                rhs=w_codes[:, cg, 2 * BANK * n : 2 * BANK * (n + 1)].bitcast(FP4X4),
                rhs_scale=w_plane[:, wg, BANK * n : BANK * (n + 1)],
                start=(g == 0),
                stop=(g == PASSES - 1),
            )

        def mx(tau):
            open_acc(tau)
            for n in range(2):
                for g in range(PASSES):
                    mx_pass(tau, n, g)

        def add_bias(tau):
            y[tau] = y_pool.tile([P, CHANNELS], F32, name="y_t", tag="y_t", align_bytes=64)
            st[tau] = st_pool.tile([P, 8], F32, name="st_t", tag="st_t")
            for n in range(2):
                cols = slice(BANK * n, BANK * (n + 1))
                nc.vector.scalar_tensor_tensor(
                    out=y[tau][:, cols],
                    in0=acc[(tau, n)][:],
                    scalar=1.0,
                    in1=b_bc[:, cols],
                    op0=ALU.mult,
                    op1=ALU.add,
                    accum_out=st[tau][:, n : n + 1],
                )
            nc.vector.scalar_tensor_tensor(
                out=st[tau][:, 2:3],
                in0=st[tau][:, 0:1],
                scalar=st[tau][:, 1:2],
                in1=cneg[:],
                op0=ALU.add,
                op1=ALU.mult,
            )

        def deviation(tau):
            sq = sq_pool.tile([P, CHANNELS], BF16, name="sq_t", tag="sq_t")
            nc.scalar.activation(
                out=sq[:], in_=y[tau][:], func=ACT.Square, bias=st[tau][:, 2:3], scale=1.0, accum_out=st[tau][:, 3:4]
            )
            nc.scalar.activation(
                out=st[tau][:, 5:6], in_=st[tau][:, 3:4], func=ACT.Abs_reciprocal_sqrt, bias=one[:], scale=s2e[:]
            )

        def normalise(tau, parts):
            width = CHANNELS // parts
            t[tau] = []
            for k in range(parts):
                part = t_pool.tile([P, width], F32, name="t_t", tag="t_t", align_bytes=64)
                nc.vector.tensor_scalar(
                    out=part[:],
                    in0=y[tau][:, width * k : width * (k + 1)],
                    scalar1=st[tau][:, 2:3],
                    scalar2=st[tau][:, 5:6],
                    op0=ALU.add,
                    op1=ALU.mult,
                )
                t[tau].append(part)

        def transposes(i, halves):
            tp[i] = []
            for k in range(4):
                tp[i].append(psum.tile([P, 2, IMG_PIX], F32, name="bank", tag="bank"))
                for j in range(2):
                    ct = 2 * k + j
                    for h in halves:
                        parts = t[2 * i + h]
                        per = CT // len(parts)
                        nc.tensor.transpose(
                            tp[i][k][:, j, P * h : P * (h + 1)],
                            parts[ct // per][:, P * (ct % per) : P * (ct % per + 1)],
                            ident[:],
                        )

        def finish(i, halves, stores):
            cols = slice(P * halves[0], P * (halves[-1] + 1))
            if halves[0] == 0:
                o[i] = o_pool.tile([P, CT, IMG_PIX], F32, name="o_t", tag="o_t")
            for ct in range(CT):
                nc.vector.scalar_tensor_tensor(
                    out=o[i][:, ct, cols],
                    in0=tp[i][ct // 2][:, ct % 2, cols],
                    scalar=wv[:, ct : ct + 1],
                    in1=x_tiles[i][:, ct, cols],
                    op0=ALU.mult,
                    op1=ALU.add,
                )
            per = CT // stores
            for k in range(stores):
                for ct in range(per * k, per * (k + 1)):
                    nc.scalar.activation(
                        out=o[i][:, ct, cols], in_=o[i][:, ct, cols], func=ACT.Relu, bias=bv[:, ct : ct + 1], scale=1.0
                    )
                nc.sync.dma_start(
                    out=out[i].rearrange("(ct p) h w -> p ct (h w)", p=P)[:, per * k : per * (k + 1), cols],
                    in_=o[i][:, per * k : per * (k + 1), cols],
                )

        idle_out = psum.tile([P, BANK], F32, name="bank", tag="bank")
        for k in range(5):
            nc.tensor.matmul(out=idle_out[:], lhsT=ones[:], rhs=idle_rhs[:], start=True, stop=True)
        open_acc(0)
        open_acc(1)
        for g in range(PASSES):
            if g == 6:
                vt = psum.tile([P, 32], F32, name="bank", tag="bank")
                nc.tensor.matmul(out=vt[:], lhsT=vrows[:], rhs=ident_bf[:], start=True, stop=True)
            for tau in range(2):
                for n in range(2):
                    mx_pass(tau, n, g)
        add_bias(0)
        deviation(0)
        add_bias(1)
        deviation(1)
        normalise(0, 1)
        normalise(1, 1)
        nc.vector.tensor_scalar(
            out=wv[:], in0=vt[:, 0:CT], scalar1=ssn[:], scalar2=EPS**-0.5, op0=ALU.mult, op1=ALU.mult
        )
        nc.vector.tensor_scalar_mul(out=bv[:], in0=vt[:, CT : 2 * CT], scalar1=sn_bf[:])

        ring = [{"done": True} for k in range(8)]
        todo = []
        slow = []
        late = []
        at = {"todo": 0, "slow": 0, "drain": 0}

        def pending():
            return at["todo"] < len(todo) or at["slow"] < len(slow)

        def drain_one():
            assert pending()
            if at["todo"] < len(todo):
                at["todo"] += 1
                todo[at["todo"] - 1]()
            else:
                at["slow"] += 1
                slow[at["slow"] - 1]()

        def drain(pieces):
            at["drain"] += 1
            for when, piece in list(late):
                if when <= at["drain"]:
                    late.remove((when, piece))
                    piece()
            for k in range(pieces):
                if pending():
                    drain_one()

        def flush_late():
            for when, piece in list(late):
                late.remove((when, piece))
                piece()

        def bank(shape):
            before = ring[len(ring) - 8]
            while not before["done"]:
                drain_one()
            ring.append({"done": False})
            return psum.tile(shape, F32, name="bank", tag="bank"), ring[len(ring) - 1]

        recs = {}
        normalised = {}

        y_read = {}

        def open_tile(tau):
            for n in range(2):
                acc[(tau, n)], recs[(tau, n)] = bank([P, BANK])
            while tau >= 6 and not y_read.get(tau - 4, False):
                drain_one()
            y[tau] = y_pool.tile([P, CHANNELS], F32, name="y_t", tag="y_t", align_bytes=64)
            st[tau] = st_pool.tile([P, 8], F32, name="st_t", tag="st_t")

        def need_normalised(images):
            for i in images:
                for h in range(2):
                    while not normalised.get(2 * i + h, False):
                        drain_one()

        def mx_tile(tau):
            open_tile(tau)
            for n in range(2):
                for g in range(PASSES):
                    mx_pass(tau, n, g)
                bias_bank(tau, n)
                recs[(tau, n)]["done"] = True
                if n == 1:
                    mean(tau)
                    deviation(tau)
                    if tau // 2 in MOVED:
                        nc.scalar.activation(
                            out=st[tau][:, 6:7], in_=st[tau][:, 5:6], func=ACT.Copy, scale=s_eps[:]
                        )
                    elif tau < 2 * (IMAGES - 1):
                        normalise_on_scalar(tau)
                    if tau in runs:
                        need_normalised(runs[tau])
                        turn_images(runs[tau])
                drain(PIECES)
            queue_post(tau)

        def bias_bank(tau, n):
            cols = slice(BANK * n, BANK * (n + 1))
            nc.vector.scalar_tensor_tensor(
                out=y[tau][:, cols],
                in0=acc[(tau, n)][:],
                scalar=1.0,
                in1=b_bc[:, cols],
                op0=ALU.mult,
                op1=ALU.add,
                accum_out=st[tau][:, n : n + 1],
            )

        def mean(tau):
            nc.scalar.activation(
                out=two[:], in_=st[tau][:, 0:2], func=ACT.Copy, scale=-1.0 / CHANNELS, accum_out=st[tau][:, 2:3]
            )

        def queue_post(tau):
            if tau // 2 in MOVED:
                queue_moved(tau)
            elif tau >= 2 * (IMAGES - 1):
                todo.append(lambda: normalise_piece(tau))

        def normalise_on_scalar(tau):
            nc.scalar.activation(out=st[tau][:, 6:7], in_=st[tau][:, 2:3], func=ACT.Copy, scale=st[tau][:, 5:6])
            part = t_pool.tile([P, CHANNELS], F32, name="t_t", tag="t_t", align_bytes=64)
            nc.scalar.activation(
                out=part[:], in_=y[tau][:], func=ACT.Identity, bias=st[tau][:, 6:7], scale=st[tau][:, 5:6]
            )
            t[tau] = [part]
            normalised[tau] = True
            y_read[tau] = True

        def normalise_piece(tau):
            normalise(tau, 1)
            normalised[tau] = True
            y_read[tau] = True

        def queue_moved(tau):
            halves = (slice(0, BANK), slice(BANK, CHANNELS))
            u = {}

            def gain(cols):
                nc.vector.scalar_tensor_tensor(
                    out=y[tau][:, cols], in0=y[tau][:, cols], scalar=st[tau][:, 2:3], in1=lw_bc[:, cols],
                    op0=ALU.add, op1=ALU.mult,
                )

            def shift(cols):
                nc.vector.scalar_tensor_tensor(
                    out=y[tau][:, cols], in0=y[tau][:, cols], scalar=st[tau][:, 6:7], in1=lb_bc[:, cols],
                    op0=ALU.mult, op1=ALU.add,
                )

            def turn(cols):
                if cols.start == 0:
                    u[0] = u_pool.tile([P, CHANNELS], F32, name="u_t", tag="u_t", align_bytes=64)
                nc.vector.transpose(out=u[0][:, cols], in_=y[tau][:, cols])
                if cols.start != 0:
                    y_read[tau] = True

            def add_x(cols):
                nc.vector.scalar_tensor_tensor(
                    out=u[0][:, cols], in0=u[0][:, cols], scalar=sn_f[:], in1=xq_tiles[tau][:, cols],
                    op0=ALU.mult, op1=ALU.add,
                )
                if cols.start != 0:
                    late.append((at["drain"] + 1, leave))

            def leave():
                nc.scalar.activation(out=u[0][:], in_=u[0][:], func=ACT.Relu)
                for a in range(4):
                    nc.sync.dma_start(
                        out=quadrant_view(out[tau // 2], tau, a),
                        in_=u[0][BLK * a : BLK * (a + 1), :].rearrange("p (b r) -> p b r", r=BLK),
                    )
                load_next_xq()

            for step in (gain, shift, turn, add_x):
                for cols in halves:
                    slow.append(lambda step=step, cols=cols: step(cols))

        def turn_images(images):
            for i in images:
                tp[i] = []
                tp_recs = []
                for k in range(4):
                    tile_k, rec_k = bank([P, 2, IMG_PIX])
                    tp[i].append(tile_k)
                    tp_recs.append(rec_k)
                    for j in range(2):
                        ct = 2 * k + j
                        for h in range(2):
                            nc.tensor.transpose(
                                tp[i][k][:, j, P * h : P * (h + 1)], t[2 * i + h][0][:, P * ct : P * (ct + 1)], ident[:]
                            )
                for k in range(4):
                    todo.append(lambda i=i, k=k, rec=tp_recs[k]: finish_bank(i, k, rec))

        def finish_bank(i, k, rec):
            if k == 0:
                o[i] = o_pool.tile([P, CT, IMG_PIX], F32, name="o_t", tag="o_t")
            for ct in (2 * k, 2 * k + 1):
                nc.vector.scalar_tensor_tensor(
                    out=o[i][:, ct, :],
                    in0=tp[i][k][:, ct % 2, :],
                    scalar=wv[:, ct : ct + 1],
                    in1=x_tiles[i][:, ct, :],
                    op0=ALU.mult,
                    op1=ALU.add,
                )
            rec["done"] = True
            for ct in (2 * k, 2 * k + 1):
                nc.scalar.activation(
                    out=o[i][:, ct, :], in_=o[i][:, ct, :], func=ACT.Relu, bias=bv[:, ct : ct + 1], scale=1.0
                )
            if k == 3:
                nc.sync.dma_start(out=out[i].rearrange("(ct p) h w -> p ct (h w)", p=P), in_=o[i][:])
                load_next_x()

        runs = {}
        plain = [i for i in range(IMAGES - 2) if i not in MOVED]
        k = 0
        while k < len(plain):
            if k + 1 < len(plain) and plain[k + 1] == plain[k] + 1 and plain[k + 1] < IMAGES - 4:
                runs[2 * plain[k + 1] + 3] = (plain[k], plain[k + 1])
                k += 2
            else:
                runs[2 * plain[k] + 3] = (plain[k],)
                k += 1

        last = IMAGES - 1
        normalised[0] = True
        normalised[1] = True
        for tau in range(2, 2 * last):
            mx_tile(tau)
            if tau == 2 * (CHUNKS[AGAIN[1]][0] + CHUNKS[AGAIN[1]][1]) - 1:
                load_h_scales(AGAIN[0], 0)
                load_h_codes(AGAIN[0])

        tau = 2 * last
        open_tile(tau)
        for n in range(2):
            for g in range(PASSES):
                mx_pass(tau, n, g)
            bias_bank(tau, n)
            recs[(tau, n)]["done"] = True
            if n == 0:
                drain(PIECES)
        mean(tau)
        deviation(tau)
        need_normalised((last - 1,))
        turn_images((last - 1,))
        while pending():
            drain_one()
        flush_late()
        normalise(tau, 1)
        tau = 2 * last + 1
        open_tile(tau)
        for n in range(2):
            for g in range(PASSES):
                mx_pass(tau, n, g)
            bias_bank(tau, n)
        mean(tau)
        deviation(tau)
        transposes(last, (0,))
        finish(last, (0,), 1)
        normalise(tau, 2)
        transposes(last, (1,))
        finish(last, (1,), 4)
